import numpy as np
import ml_dtypes


def mxq(x, axis, fmt="e4m3"):
    dtype, down = {"e4m3": (ml_dtypes.float8_e4m3fn, 7), "e5m2": (ml_dtypes.float8_e5m2, 14)}[fmt]
    v = np.moveaxis(np.asarray(x, np.float32).astype(ml_dtypes.bfloat16).astype(np.float64), axis, -1)
    blocks = v.reshape(v.shape[:-1] + (-1, 32))
    amax = np.abs(blocks).max(-1, keepdims=True)
    byte = np.maximum(np.where(amax > 0, np.frexp(amax)[1] - 1 + 127, 0) - down, 1)
    scale = np.exp2(byte - 127.0)
    codes = (blocks / scale).astype(np.float32).astype(dtype).astype(np.float64)
    return np.moveaxis((codes * scale).reshape(v.shape), -1, axis)


WIDE = False


def mx_kscale(k):
    if not WIDE:
        return np.ones(k)
    levels = np.array([10, -10, 5, -5, 0])
    a = np.random.permutation(np.resize(levels, k // 512 * 4)).reshape(k // 512, 4)
    idx = np.arange(k)
    return np.exp2(a[idx // 512, idx % 128 // 32])


BF16 = ml_dtypes.bfloat16


def bf(x):
    return np.asarray(x, np.float32).astype(BF16)


def f64(x):
    return np.asarray(x).astype(np.float64)


B, N, R, DE, DR, NUM_BASES, OUT_DIM = 8, 512, 4, 64, 64, 1024, 128
F = DE + DR
KS = R * F


def setup_inputs():
    s = mx_kscale(N)
    t = mx_kscale(KS)[:F]
    deg = np.random.uniform(0.5, 1.5, (B, R, N, 1))
    adj = np.random.uniform(0.0, 1.0, (B, R, N, N)) * deg / np.sqrt(N)
    return {"node_features": bf(np.random.standard_normal((B, N, DE)) * 2.0 / s[:, None] * t[:DE]),
            "relation_features": bf(np.random.standard_normal((B, R, DR)) * 2.0 / np.sqrt(N) / s.mean() * t[DE:]),
            "adj": bf(adj * s),
            "Wb": bf(np.random.standard_normal((NUM_BASES, KS)) / np.sqrt(KS) / np.tile(t, R))}


def reference(node_features, relation_features, adj, Wb):
    a = f64(adj)
    node_part = mxq(a, 3, "e4m3") @ mxq(f64(node_features), 1, "e4m3")[:, None]
    row_sum = a.sum(-1)
    rel_part = row_sum[..., None] * f64(relation_features)[:, :, None, :]
    supports = np.concatenate([node_part, rel_part], -1)
    supports = supports.transpose(0, 2, 1, 3).reshape(B, N, KS)
    return mxq(supports, 2, "e4m3") @ mxq(f64(Wb), 1, "e4m3").T

@@ -1,0 +1,318 @@
+from contextlib import ExitStack
+
+import concourse.bass as bass
+import concourse.mybir as mybir
+import concourse.tile as tile
+from concourse.masks import make_identity
+
+FLOPS = 2 * 8 * 4 * 512 * 512 * 64 + 2 * 8 * 512 * 512 * 1024
+
+BF16 = mybir.dt.bfloat16
+F32 = mybir.dt.float32
+U32 = mybir.dt.uint32
+U8 = mybir.dt.uint8
+I32 = mybir.dt.int32
+FP8X4 = mybir.dt.float8_e4m3fn_x4
+MULT = mybir.AluOpType.mult
+ADD = mybir.AluOpType.add
+
+P = 128
+NB = 8
+NR = 4
+NT = 4
+NU = NB * NT
+LD = 6
+MANUAL = True
+V_D1_FROM = 25
+
+
+def tile_relationalgraphconvolution_pa_t_kernel(tc, node_features, relation_features, adj, Wb, out):
+    nc = tc.nc
+    with ExitStack() as ctx:
+        const = ctx.enter_context(tc.tile_pool(name="const", bufs=1))
+        work = ctx.enter_context(tc.tile_pool(name="work", bufs=2))
+        psum = ctx.enter_context(tc.psum_pool(name="psum", bufs=1))
+        if MANUAL:
+            ctx.enter_context(tc.manual_schedule())
+
+        adj_sb = []
+        for b in range(NB):
+            adj_t = const.tile([P, NR * NT * 512], BF16, name="adj%d" % b)
+            adj_sb.append(adj_t)
+
+        def load_it(b, it):
+            nc.sync.dma_start(
+                out=adj_sb[b][:].rearrange("p (r t j) -> p r t j", r=NR, t=NT)[:, :, it, :],
+                in_=adj[b].rearrange("r (p t) j -> p r t j", t=NT)[:, :, it, :],
+            )
+
+        def load_r(b, r):
+            nc.sync.dma_start(
+                out=adj_sb[b][:, r * 2048:(r + 1) * 2048],
+                in_=adj[b, r].rearrange("(p t) j -> p (t j)", t=NT),
+            )
+
+        nfraw = const.tile([P, 2048], BF16, name="nfraw")
+        nfg = const.tile([P, 2048], BF16, name="nfg", align_bytes=64)
+        nfc = const.tile([P, NB * 128], U32, name="nfc", align_bytes=64)
+        nfs = const.tile([P, NB * 128], U8, name="nfs", align_bytes=64)
+        relz = const.tile([P, P], BF16, name="relz")
+        relcol = const.tile([P, NB * NR], F32, name="relcol")
+        identf = const.tile([P, P], F32, name="identf")
+        identb = const.tile([P, P], BF16, name="identb")
+        wb_sb = const.tile([P, 4096], BF16, name="wb_sb")
+        wbg = const.tile([P, 4096], BF16, name="wbg", align_bytes=64)
+        wbc = const.tile([P, 1024], U32, name="wbc", align_bytes=64)
+        wbs = const.tile([P, 1024], U8, name="wbs", align_bytes=64)
+
+        load_it(0, 0)
+        nc.vector.memset(relz[:], 0.0)
+        nc.scalar.dma_start(
+            out=nfraw[:, 0:256].rearrange("q (u x) -> q u x", u=2),
+            in_=node_features[0].rearrange("(u q e) d -> q u (e d)", u=2, e=2),
+        )
+        nc.scalar.dma_start(out=relz[0:32, 64:128], in_=relation_features.rearrange("b r f -> (b r) f"))
+        load_it(0, 1)
+        nc.sync.dma_start(
+            out=wb_sb[:].rearrange("p (t k) -> p t k", t=8),
+            in_=Wb.rearrange("(t p) k -> p t k", p=P),
+        )
+        load_it(0, 2)
+        load_it(0, 3)
+        nc.sync.dma_start(
+            out=nfraw[:, 256:2048].rearrange("q (c x) -> q c x", c=14),
+            in_=node_features[1:8].rearrange("b (u q e) d -> q (b u) (e d)", u=2, e=2),
+        )
+        for it in range(NT):
+            load_it(1, it)
+
+        make_identity(nc, identf[:])
+        make_identity(nc, identb[:])
+        nc.vector.memset(nfc[:].bitcast(I32), 0)
+        nc.vector.memset(nfs[:].bitcast(I32), 0)
+
+        def quant_nf(b):
+            nc.vector.quantize_mx(
+                out=nfc[:, b * 128:b * 128 + 64].bitcast(FP8X4),
+                scales=nfs[:, b * 128:b * 128 + 64],
+                in_=nfg[:, b * 256:(b + 1) * 256],
+            )
+
+        nc.vector.tensor_copy(
+            out=nfg[:, 0:256].rearrange("q (d t) -> q d t", t=4),
+            in_=nfraw[:, 0:256].rearrange("q (t d) -> q d t", t=4),
+        )
+
+        st = {"rs": {}, "A": {}, "grp": {}, "cA": {}, "sA": {}, "N": {}, "R": {}, "g2": {}, "c2": {}, "s2": {}, "D": {}}
+
+        def stt(u, rlist):
+            b, it = divmod(u, NT)
+            if u not in st["rs"]:
+                rs = work.tile([P, NR], F32, tag="rs", bufs=3)
+                st["rs"][u] = rs
+            rs = st["rs"][u]
+            for r in rlist:
+                base = (r * NT + it) * 512
+                junk = work.tile([P, 256], F32, tag="junk", bufs=2)
+                nc.vector.scalar_tensor_tensor(
+                    out=junk[:],
+                    in0=adj_sb[b][:, base:base + 256],
+                    scalar=1.0,
+                    in1=adj_sb[b][:, base + 256:base + 512],
+                    op0=MULT,
+                    op1=ADD,
+                    accum_out=rs[:, r:r + 1],
+                )
+
+        def a_tr(u):
+            b, it = divmod(u, NT)
+            adjw = adj_sb[b][:].bitcast(F32)
+            banks = []
+            for h in range(2):
+                bank_a = psum.tile([P, 512], F32, tag="A", bufs=2)
+                for rr in range(2):
+                    for uu in range(2):
+                        col = ((2 * h + rr) * NT + it) * 256 + 128 * uu
+                        nc.tensor.transpose(
+                            bank_a[:, (rr * 2 + uu) * 128:(rr * 2 + uu + 1) * 128],
+                            adjw[:, col:col + 128],
+                            identf[:],
+                        )
+                banks.append(bank_a)
+            st["A"][u] = banks
+
+        def a_exit(u):
+            grp = work.tile([P, 2048], BF16, tag="grp", bufs=3, align_bytes=64)
+            st["grp"][u] = grp
+            gw = grp[:].bitcast(F32)
+            for h in range(2):
+                nc.scalar.copy(
+                    out=gw[:, h * 512:(h + 1) * 512].rearrange("p (rr i u) -> p rr i u", rr=2, u=2),
+                    in_=st["A"][u][h][:].rearrange("p (rr u i) -> p rr i u", rr=2, u=2),
+                )
+
+        def q_a(u):
+            c_a = work.tile([P, 512], U32, tag="cA", bufs=3, align_bytes=64)
+            s_a = work.tile([P, 512], U8, tag="sA", bufs=3, align_bytes=64)
+            st["cA"][u] = c_a
+            st["sA"][u] = s_a
+            nc.vector.quantize_mx(out=c_a[:].bitcast(FP8X4), scales=s_a[:], in_=st["grp"][u][:])
+
+        def b_mm(u):
+            b, it = divmod(u, NT)
+            bank_n = psum.tile([P, 512], F32, tag="N", bufs=1)
+            st["N"][u] = bank_n
+            nc.tensor.matmul_mx(
+                out=bank_n[:],
+                lhsT=nfc[:, b * 128:(b + 1) * 128].bitcast(FP8X4),
+                lhsT_scale=nfs[:, b * 128:(b + 1) * 128],
+                rhs=st["cA"][u][:].bitcast(FP8X4),
+                rhs_scale=st["sA"][u][:],
+                start=True,
+                stop=True,
+            )
+
+        def r_tr(u):
+            bank_r = psum.tile([P, 512], F32, tag="R", bufs=1)
+            st["R"][u] = bank_r
+            rs = st["rs"][u]
+            for r in range(NR):
+                nc.tensor.transpose(
+                    bank_r[:, r * 128:(r + 1) * 128],
+                    rs[:, r:r + 1].to_broadcast([P, P]),
+                    identf[:],
+                )
+
+        def get_g2(u):
+            if u not in st["g2"]:
+                g2 = work.tile([P, 512], BF16, tag="g2", bufs=3, align_bytes=64)
+                st["g2"][u] = g2
+            return st["g2"][u]
+
+        def n_exit(u):
+            g2 = get_g2(u)
+            nc.scalar.copy(
+                out=g2[0:64, :].rearrange("p (i r) -> p i r", r=NR),
+                in_=st["N"][u][0:64, :].rearrange("p (r i) -> p i r", r=NR),
+            )
+
+        def rel_exit(u):
+            b, it = divmod(u, NT)
+            g2 = get_g2(u)
+            nc.vector.tensor_tensor(
+                out=g2[64:128, :].rearrange("p (i r) -> p i r", r=NR),
+                in0=st["R"][u][64:128, :].rearrange("p (r i) -> p i r", r=NR),
+                in1=relcol[64:128, NR * b:NR * (b + 1)].unsqueeze(1).to_broadcast([64, P, NR]),
+                op=MULT,
+            )
+
+        def q_s(u):
+            c_2 = work.tile([P, P], U32, tag="c2", bufs=LD + 2, align_bytes=64)
+            s_2 = work.tile([P, P], U8, tag="s2", bufs=LD + 2, align_bytes=64)
+            st["c2"][u] = c_2
+            st["s2"][u] = s_2
+            nc.vector.quantize_mx(out=c_2[:].bitcast(FP8X4), scales=s_2[:], in_=st["g2"][u][:])
+
+        def d_mm(u):
+            banks = []
+            for h in range(2):
+                bank_d = psum.tile([P, 512], F32, tag="D", bufs=2)
+                nc.tensor.matmul_mx(
+                    out=bank_d[:],
+                    lhsT=st["c2"][u][:].bitcast(FP8X4),
+                    lhsT_scale=st["s2"][u][:],
+                    rhs=wbc[:, h * 512:(h + 1) * 512].bitcast(FP8X4),
+                    rhs_scale=wbs[:, h * 512:(h + 1) * 512],
+                    start=True,
+                    stop=True,
+                )
+                banks.append(bank_d)
+            st["D"][u] = banks
+
+        def d_exit(u):
+            b, it = divmod(u, NT)
+            ost = work.tile([P, 1024], F32, tag="ost", bufs=4)
+            nc.scalar.copy(out=ost[:, 0:512], in_=st["D"][u][0][:])
+            if u >= V_D1_FROM:
+                nc.vector.tensor_copy(out=ost[:, 512:1024], in_=st["D"][u][1][:])
+            else:
+                nc.scalar.copy(out=ost[:, 512:1024], in_=st["D"][u][1][:])
+            nc.sync.dma_start(out=out[b].rearrange("(p t) n -> p t n", t=NT)[:, it, :], in_=ost[:])
+
+        wbank = {}
+
+        def wb_tr(g):
+            bank_w = psum.tile([P, 1024], BF16, tag="D", bufs=2)
+            wbank[g] = bank_w
+            for nn in range(2):
+                for t in range(4):
+                    nc.tensor.transpose(
+                        bank_w[:, (nn * 4 + t) * 128:(nn * 4 + t + 1) * 128],
+                        wb_sb[:, (2 * g + nn) * 512 + t * 128:(2 * g + nn) * 512 + (t + 1) * 128],
+                        identb[:],
+                    )
+
+        def wb_exit(g):
+            nc.scalar.copy(
+                out=wbg[:, g * 1024:(g + 1) * 1024].rearrange("p (nn n t) -> p nn n t", nn=2, t=4),
+                in_=wbank[g][:].rearrange("p (nn t n) -> p nn n t", nn=2, t=4),
+            )
+
+        def wb_quant(h):
+            nc.vector.quantize_mx(
+                out=wbc[:, h * 512:(h + 1) * 512].bitcast(FP8X4),
+                scales=wbs[:, h * 512:(h + 1) * 512],
+                in_=wbg[:, h * 2048:(h + 1) * 2048],
+            )
+
+        bank_t = psum.tile([P, P], BF16, tag="R", bufs=1)
+        nc.tensor.transpose(bank_t[:], relz[:], identb[:])
+        nc.vector.tensor_copy(out=relcol[:], in_=bank_t[:, 0:NB * NR])
+        quant_nf(0)
+
+        def ok(u):
+            return 0 <= u < NU
+
+        for k in range(NU + LD + 2):
+            if k < 24:
+                load_r(2 + k // 4, k % 4)
+            if ok(k - LD - 1):
+                d_exit(k - LD - 1)
+            if ok(k - 2):
+                q_s(k - 2)
+            if ok(k - 1):
+                q_a(k - 1)
+            if k == 4:
+                wb_quant(0)
+            if k == 6:
+                wb_quant(1)
+            if k == 4:
+                for b in range(1, NB):
+                    quant_nf(b)
+            if ok(k):
+                a_tr(k)
+            if ok(k - 1):
+                r_tr(k - 1)
+            if 2 <= k < 6:
+                wb_tr(k - 2)
+            if ok(k):
+                stt(k, [0, 1])
+            if ok(k - 1):
+                b_mm(k - 1)
+            if ok(k - LD):
+                d_mm(k - LD)
+            if ok(k):
+                a_exit(k)
+            if ok(k - 1):
+                rel_exit(k - 1)
+            if ok(k):
+                stt(k, [2, 3])
+            if ok(k - 1):
+                n_exit(k - 1)
+            if 2 <= k < 6:
+                wb_exit(k - 2)
+            if k == 3:
+                nc.scalar.copy(
+                    out=nfg[:, 256:2048].rearrange("q (b d t) -> q b d t", b=7, t=4),
+                    in_=nfraw[:, 256:2048].rearrange("q (b t d) -> q b d t", b=7, t=4),
+                )

@@ -21,9 +21,10 @@ NB = 8
 NR = 4
 NT = 4
 NU = NB * NT
-LD = 6
+LD = 5
 MANUAL = True
-V_D1_FROM = 25
+V_D1_FROM = 27
+NP = 31
 
 
 def tile_relationalgraphconvolution_pa_t_kernel(tc, node_features, relation_features, adj, Wb, out):
@@ -65,19 +66,23 @@ def tile_relationalgraphconvolution_pa_t_kernel(tc, node_features, relation_feat
         wbc = const.tile([P, 1024], U32, name="wbc", align_bytes=64)
         wbs = const.tile([P, 1024], U8, name="wbs", align_bytes=64)
 
-        load_it(0, 0)
+        zc = const.tile([P, 512], U32, name="zc", align_bytes=64)
+        zs = const.tile([P, 512], U8, name="zs", align_bytes=64)
+        zb = const.tile([P, 2048], BF16, name="zb", align_bytes=64)
+        nc.vector.memset(zb[:].bitcast(I32), 0)
+        nc.vector.quantize_mx(out=zc[:].bitcast(FP8X4), scales=zs[:], in_=zb[:])
         nc.vector.memset(relz[:], 0.0)
-        nc.scalar.dma_start(
+        load_it(0, 0)
+        nc.sync.dma_start(
             out=nfraw[:, 0:256].rearrange("q (u x) -> q u x", u=2),
             in_=node_features[0].rearrange("(u q e) d -> q u (e d)", u=2, e=2),
         )
-        nc.scalar.dma_start(out=relz[0:32, 64:128], in_=relation_features.rearrange("b r f -> (b r) f"))
+        nc.sync.dma_start(out=relz[0:32, 64:128], in_=relation_features.rearrange("b r f -> (b r) f"))
         load_it(0, 1)
-        nc.sync.dma_start(
-            out=wb_sb[:].rearrange("p (t k) -> p t k", t=8),
-            in_=Wb.rearrange("(t p) k -> p t k", p=P),
-        )
+        wb_view = Wb.rearrange("(t p) k -> p t k", p=P)
+        nc.sync.dma_start(out=wb_sb[:, 0:2048].rearrange("p (t k) -> p t k", t=4), in_=wb_view[:, 0:4, :])
         load_it(0, 2)
+        nc.sync.dma_start(out=wb_sb[:, 2048:4096].rearrange("p (t k) -> p t k", t=4), in_=wb_view[:, 4:8, :])
         load_it(0, 3)
         nc.sync.dma_start(
             out=nfraw[:, 256:2048].rearrange("q (c x) -> q c x", c=14),
@@ -98,12 +103,7 @@ def tile_relationalgraphconvolution_pa_t_kernel(tc, node_features, relation_feat
                 in_=nfg[:, b * 256:(b + 1) * 256],
             )
 
-        nc.vector.tensor_copy(
-            out=nfg[:, 0:256].rearrange("q (d t) -> q d t", t=4),
-            in_=nfraw[:, 0:256].rearrange("q (t d) -> q d t", t=4),
-        )
-
-        st = {"rs": {}, "A": {}, "grp": {}, "cA": {}, "sA": {}, "N": {}, "R": {}, "g2": {}, "c2": {}, "s2": {}, "D": {}}
+        st = {"rs": {}, "A": {}, "grp": {}, "cA": {}, "sA": {}, "N": {}, "R": {}, "g2": {}, "c2": {}, "s2": {}, "D": {}, "P": {}}
 
         def stt(u, rlist):
             b, it = divmod(u, NT)
@@ -124,32 +124,65 @@ def tile_relationalgraphconvolution_pa_t_kernel(tc, node_features, relation_feat
                     accum_out=rs[:, r:r + 1],
                 )
 
-        def a_tr(u):
+        def a_tr(u, h):
             b, it = divmod(u, NT)
             adjw = adj_sb[b][:].bitcast(F32)
-            banks = []
-            for h in range(2):
-                bank_a = psum.tile([P, 512], F32, tag="A", bufs=2)
-                for rr in range(2):
-                    for uu in range(2):
-                        col = ((2 * h + rr) * NT + it) * 256 + 128 * uu
-                        nc.tensor.transpose(
-                            bank_a[:, (rr * 2 + uu) * 128:(rr * 2 + uu + 1) * 128],
-                            adjw[:, col:col + 128],
-                            identf[:],
-                        )
-                banks.append(bank_a)
-            st["A"][u] = banks
+            bank_a = psum.tile([P, 512], F32, tag="A", bufs=2)
+            for rr in range(2):
+                for uu in range(2):
+                    col = ((2 * h + rr) * NT + it) * 256 + 128 * uu
+                    nc.tensor.transpose(
+                        bank_a[:, (rr * 2 + uu) * 128:(rr * 2 + uu + 1) * 128],
+                        adjw[:, col:col + 128],
+                        identf[:],
+                    )
+            st["A"][(u, h)] = bank_a
 
-        def a_exit(u):
-            grp = work.tile([P, 2048], BF16, tag="grp", bufs=3, align_bytes=64)
-            st["grp"][u] = grp
-            gw = grp[:].bitcast(F32)
-            for h in range(2):
-                nc.scalar.copy(
-                    out=gw[:, h * 512:(h + 1) * 512].rearrange("p (rr i u) -> p rr i u", rr=2, u=2),
-                    in_=st["A"][u][h][:].rearrange("p (rr u i) -> p rr i u", rr=2, u=2),
+        def a_exit(u, h):
+            if u not in st["grp"]:
+                grp = work.tile([P, 2048], BF16, tag="grp", bufs=3, align_bytes=64)
+                st["grp"][u] = grp
+            gw = st["grp"][u][:].bitcast(F32)
+            nc.scalar.copy(
+                out=gw[:, h * 512:(h + 1) * 512].rearrange("p (rr i u) -> p rr i u", rr=2, u=2),
+                in_=st["A"][(u, h)][:].rearrange("p (rr u i) -> p rr i u", rr=2, u=2),
+            )
+
+        def p_mm(u):
+            b, it = divmod(u, NT)
+            base = (3 * NT + it) * 512
+            bank_p = psum.tile([P, 64], F32, tag="P", bufs=1)
+            st["P"][u] = bank_p
+            for c in range(8):
+                nc.tensor.matmul(
+                    out=bank_p[:],
+                    lhsT=identb[:],
+                    rhs=adj_sb[b][:, base + 64 * c:base + 64 * (c + 1)],
+                    start=(c == 0),
+                    stop=(c == 7),
                 )
+
+        def p_red(u):
+            nc.vector.tensor_reduce(out=st["rs"][u][:, 3:4], in_=st["P"][u][:], axis=mybir.AxisListType.X, op=ADD)
+
+        def dummy(n):
+            for i in range(n):
+                bank_x = psum.tile([P, 512], F32, tag="X", bufs=1)
+                nc.tensor.matmul_mx(
+                    out=bank_x[:],
+                    lhsT=zc[:, 0:128].bitcast(FP8X4),
+                    lhsT_scale=zs[:, 0:128],
+                    rhs=zc[:].bitcast(FP8X4),
+                    rhs_scale=zs[:],
+                    start=True,
+                    stop=True,
+                )
+
+        def nf_regroup(b):
+            nc.scalar.copy(
+                out=nfg[:, b * 256:(b + 1) * 256].rearrange("q (d t) -> q d t", t=4),
+                in_=nfraw[:, b * 256:(b + 1) * 256].rearrange("q (t d) -> q d t", t=4),
+            )
 
         def q_a(u):
             c_a = work.tile([P, 512], U32, tag="cA", bufs=3, align_bytes=64)
@@ -233,7 +266,7 @@ def tile_relationalgraphconvolution_pa_t_kernel(tc, node_features, relation_feat
             b, it = divmod(u, NT)
             ost = work.tile([P, 1024], F32, tag="ost", bufs=4)
             nc.scalar.copy(out=ost[:, 0:512], in_=st["D"][u][0][:])
-            if u >= V_D1_FROM:
+            if u >= V_D1_FROM or u % 6 == 5:
                 nc.vector.tensor_copy(out=ost[:, 512:1024], in_=st["D"][u][1][:])
             else:
                 nc.scalar.copy(out=ost[:, 512:1024], in_=st["D"][u][1][:])
@@ -265,54 +298,68 @@ def tile_relationalgraphconvolution_pa_t_kernel(tc, node_features, relation_feat
                 in_=wbg[:, h * 2048:(h + 1) * 2048],
             )
 
-        bank_t = psum.tile([P, P], BF16, tag="R", bufs=1)
-        nc.tensor.transpose(bank_t[:], relz[:], identb[:])
-        nc.vector.tensor_copy(out=relcol[:], in_=bank_t[:, 0:NB * NR])
-        quant_nf(0)
-
         def ok(u):
             return 0 <= u < NU
 
-        for k in range(NU + LD + 2):
+        dummy(4)
+
+        for k in range(NU + LD + 1):
             if k < 24:
                 load_r(2 + k // 4, k % 4)
-            if ok(k - LD - 1):
-                d_exit(k - LD - 1)
             if ok(k - 2):
-                q_s(k - 2)
-            if ok(k - 1):
-                q_a(k - 1)
-            if k == 4:
-                wb_quant(0)
-            if k == 6:
-                wb_quant(1)
-            if k == 4:
-                for b in range(1, NB):
-                    quant_nf(b)
+                n_exit(k - 2)
             if ok(k):
-                a_tr(k)
+                stt(k, [0])
+                a_tr(k, 0)
+            if k == 1:
+                bank_t = psum.tile([P, P], BF16, tag="R", bufs=1)
+                nc.tensor.transpose(bank_t[:], relz[:], identb[:])
+                nc.vector.tensor_copy(out=relcol[:], in_=bank_t[:, 0:NB * NR])
             if ok(k - 1):
                 r_tr(k - 1)
-            if 2 <= k < 6:
-                wb_tr(k - 2)
-            if ok(k):
-                stt(k, [0, 1])
+            if k == 3:
+                wb_quant(0)
+            if k == 5:
+                wb_quant(1)
+            if k % 4 == 0 and 1 <= k // 4 < NB:
+                quant_nf(k // 4)
             if ok(k - 1):
-                b_mm(k - 1)
+                q_a(k - 1)
+            if ok(k - 2):
+                q_s(k - 2)
+            if ok(k):
+                a_exit(k, 0)
+            if k == 0:
+                nc.vector.tensor_copy(
+                    out=nfg[:, 0:256].rearrange("q (d t) -> q d t", t=4),
+                    in_=nfraw[:, 0:256].rearrange("q (t d) -> q d t", t=4),
+                )
             if ok(k - LD):
                 d_mm(k - LD)
+            elif k < LD:
+                dummy(2)
             if ok(k):
-                a_exit(k)
+                a_tr(k, 1)
+            if 1 <= k < 5:
+                wb_tr(k - 1)
             if ok(k - 1):
                 rel_exit(k - 1)
-            if ok(k):
-                stt(k, [2, 3])
+            if ok(k - LD):
+                d_exit(k - LD)
+            if ok(k) and k < NP:
+                p_mm(k)
             if ok(k - 1):
-                n_exit(k - 1)
-            if 2 <= k < 6:
-                wb_exit(k - 2)
-            if k == 3:
-                nc.scalar.copy(
-                    out=nfg[:, 256:2048].rearrange("q (b d t) -> q b d t", b=7, t=4),
-                    in_=nfraw[:, 256:2048].rearrange("q (b t d) -> q b d t", b=7, t=4),
-                )
+                b_mm(k - 1)
+            elif k == 0:
+                dummy(1)
+            if ok(k):
+                stt(k, [1, 2] if k < NP else [1, 2, 3])
+                a_exit(k, 1)
+            if 1 <= k < 5:
+                wb_exit(k - 1)
+            if k % 4 == 3 and 1 <= (k + 1) // 4 < NB:
+                nf_regroup((k + 1) // 4)
+            if ok(k) and k < NP:
+                p_red(k)
+            if k == 0:
+                quant_nf(0)

@@ -266,7 +266,7 @@ def tile_relationalgraphconvolution_pa_t_kernel(tc, node_features, relation_feat
             b, it = divmod(u, NT)
             ost = work.tile([P, 1024], F32, tag="ost", bufs=4)
             nc.scalar.copy(out=ost[:, 0:512], in_=st["D"][u][0][:])
-            if u >= V_D1_FROM or u % 6 == 5:
+            if u >= V_D1_FROM or u % 2 == 1:
                 nc.vector.tensor_copy(out=ost[:, 512:1024], in_=st["D"][u][1][:])
             else:
                 nc.scalar.copy(out=ost[:, 512:1024], in_=st["D"][u][1][:])

@@ -24,7 +24,6 @@ NU = NB * NT
 LD = 5
 MANUAL = True
 V_D1_FROM = 27
-NP = 31
 
 
 def tile_relationalgraphconvolution_pa_t_kernel(tc, node_features, relation_features, adj, Wb, out):
@@ -72,6 +71,8 @@ def tile_relationalgraphconvolution_pa_t_kernel(tc, node_features, relation_feat
         nc.vector.memset(zb[:].bitcast(I32), 0)
         nc.vector.quantize_mx(out=zc[:].bitcast(FP8X4), scales=zs[:], in_=zb[:])
         nc.vector.memset(relz[:], 0.0)
+        ones = const.tile([P, P], BF16, name="ones")
+        nc.vector.memset(ones[:], 1.0)
         load_it(0, 0)
         nc.sync.dma_start(
             out=nfraw[:, 0:256].rearrange("q (u x) -> q u x", u=2),
@@ -103,7 +104,7 @@ def tile_relationalgraphconvolution_pa_t_kernel(tc, node_features, relation_feat
                 in_=nfg[:, b * 256:(b + 1) * 256],
             )
 
-        st = {"rs": {}, "A": {}, "grp": {}, "cA": {}, "sA": {}, "N": {}, "R": {}, "g2": {}, "c2": {}, "s2": {}, "D": {}, "P": {}}
+        st = {"rs": {}, "A": {}, "grp": {}, "cA": {}, "sA": {}, "N": {}, "R": {}, "g2": {}, "c2": {}, "s2": {}, "D": {}}
 
         def stt(u, rlist):
             b, it = divmod(u, NT)
@@ -148,23 +149,6 @@ def tile_relationalgraphconvolution_pa_t_kernel(tc, node_features, relation_feat
                 in_=st["A"][(u, h)][:].rearrange("p (rr u i) -> p rr i u", rr=2, u=2),
             )
 
-        def p_mm(u):
-            b, it = divmod(u, NT)
-            base = (3 * NT + it) * 512
-            bank_p = psum.tile([P, 64], F32, tag="P", bufs=1)
-            st["P"][u] = bank_p
-            for c in range(8):
-                nc.tensor.matmul(
-                    out=bank_p[:],
-                    lhsT=identb[:],
-                    rhs=adj_sb[b][:, base + 64 * c:base + 64 * (c + 1)],
-                    start=(c == 0),
-                    stop=(c == 7),
-                )
-
-        def p_red(u):
-            nc.vector.tensor_reduce(out=st["rs"][u][:, 3:4], in_=st["P"][u][:], axis=mybir.AxisListType.X, op=ADD)
-
         def dummy(n):
             for i in range(n):
                 bank_x = psum.tile([P, 512], F32, tag="X", bufs=1)
@@ -206,14 +190,25 @@ def tile_relationalgraphconvolution_pa_t_kernel(tc, node_features, relation_feat
             )
 
         def r_tr(u):
-            bank_r = psum.tile([P, 512], F32, tag="R", bufs=1)
+            bank_r = psum.tile([P, 512], F32, tag="R", bufs=2)
             st["R"][u] = bank_r
             rs = st["rs"][u]
-            for r in range(NR):
+            for r in range(NR if u == 0 else NR - 1):
                 nc.tensor.transpose(
                     bank_r[:, r * 128:(r + 1) * 128],
                     rs[:, r:r + 1].to_broadcast([P, P]),
                     identf[:],
+                )
+
+        def r_mm(u):
+            gv = st["grp"][u][:].rearrange("p (r i t) -> p r i t", r=NR, t=4)
+            for t in range(4):
+                nc.tensor.matmul(
+                    out=st["R"][u][:, 384:512],
+                    lhsT=ones[:],
+                    rhs=gv[:, 3, :, t],
+                    start=(t == 0),
+                    stop=(t == 3),
                 )
 
         def get_g2(u):
@@ -266,7 +261,7 @@ def tile_relationalgraphconvolution_pa_t_kernel(tc, node_features, relation_feat
             b, it = divmod(u, NT)
             ost = work.tile([P, 1024], F32, tag="ost", bufs=4)
             nc.scalar.copy(out=ost[:, 0:512], in_=st["D"][u][0][:])
-            if u >= V_D1_FROM or u % 2 == 1:
+            if u >= V_D1_FROM:
                 nc.vector.tensor_copy(out=ost[:, 512:1024], in_=st["D"][u][1][:])
             else:
                 nc.scalar.copy(out=ost[:, 512:1024], in_=st["D"][u][1][:])
@@ -312,7 +307,7 @@ def tile_relationalgraphconvolution_pa_t_kernel(tc, node_features, relation_feat
                 stt(k, [0])
                 a_tr(k, 0)
             if k == 1:
-                bank_t = psum.tile([P, P], BF16, tag="R", bufs=1)
+                bank_t = psum.tile([P, P], BF16, tag="R", bufs=2)
                 nc.tensor.transpose(bank_t[:], relz[:], identb[:])
                 nc.vector.tensor_copy(out=relcol[:], in_=bank_t[:, 0:NB * NR])
             if ok(k - 1):
@@ -342,24 +337,22 @@ def tile_relationalgraphconvolution_pa_t_kernel(tc, node_features, relation_feat
                 a_tr(k, 1)
             if 1 <= k < 5:
                 wb_tr(k - 1)
-            if ok(k - 1):
-                rel_exit(k - 1)
             if ok(k - LD):
                 d_exit(k - LD)
-            if ok(k) and k < NP:
-                p_mm(k)
+            if ok(k - 1) and k - 1 > 0:
+                r_mm(k - 1)
             if ok(k - 1):
                 b_mm(k - 1)
             elif k == 0:
-                dummy(1)
+                dummy(2)
             if ok(k):
-                stt(k, [1, 2] if k < NP else [1, 2, 3])
+                stt(k, [1, 2] if k > 0 else [1, 2, 3])
                 a_exit(k, 1)
+            if ok(k - 1):
+                rel_exit(k - 1)
             if 1 <= k < 5:
                 wb_exit(k - 1)
             if k % 4 == 3 and 1 <= (k + 1) // 4 < NB:
                 nf_regroup((k + 1) // 4)
-            if ok(k) and k < NP:
-                p_red(k)
             if k == 0:
                 quant_nf(0)

@@ -109,7 +109,7 @@ def tile_relationalgraphconvolution_pa_t_kernel(tc, node_features, relation_feat
         def stt(u, rlist):
             b, it = divmod(u, NT)
             if u not in st["rs"]:
-                rs = work.tile([P, NR], F32, tag="rs", bufs=3)
+                rs = work.tile([P, NR], F32, tag="rs", bufs=4)
                 st["rs"][u] = rs
             rs = st["rs"][u]
             for r in rlist:
@@ -141,7 +141,7 @@ def tile_relationalgraphconvolution_pa_t_kernel(tc, node_features, relation_feat
 
         def a_exit(u, h):
             if u not in st["grp"]:
-                grp = work.tile([P, 2048], BF16, tag="grp", bufs=3, align_bytes=64)
+                grp = work.tile([P, 2048], BF16, tag="grp", bufs=4, align_bytes=64)
                 st["grp"][u] = grp
             gw = st["grp"][u][:].bitcast(F32)
             nc.scalar.copy(
@@ -213,7 +213,7 @@ def tile_relationalgraphconvolution_pa_t_kernel(tc, node_features, relation_feat
 
         def get_g2(u):
             if u not in st["g2"]:
-                g2 = work.tile([P, 512], BF16, tag="g2", bufs=3, align_bytes=64)
+                g2 = work.tile([P, 512], BF16, tag="g2", bufs=4, align_bytes=64)
                 st["g2"][u] = g2
             return st["g2"][u]
 
@@ -228,9 +228,9 @@ def tile_relationalgraphconvolution_pa_t_kernel(tc, node_features, relation_feat
             b, it = divmod(u, NT)
             g2 = get_g2(u)
             nc.vector.tensor_tensor(
-                out=g2[64:128, :].rearrange("p (i r) -> p i r", r=NR),
-                in0=st["R"][u][64:128, :].rearrange("p (r i) -> p i r", r=NR),
-                in1=relcol[64:128, NR * b:NR * (b + 1)].unsqueeze(1).to_broadcast([64, P, NR]),
+                out=g2[:].rearrange("p (i r) -> p i r", r=NR),
+                in0=st["R"][u][:].rearrange("p (r i) -> p i r", r=NR),
+                in1=relcol[:, NR * b:NR * (b + 1)].unsqueeze(1).to_broadcast([P, P, NR]),
                 op=MULT,
             )
 
@@ -301,8 +301,8 @@ def tile_relationalgraphconvolution_pa_t_kernel(tc, node_features, relation_feat
         for k in range(NU + LD + 1):
             if k < 24:
                 load_r(2 + k // 4, k % 4)
-            if ok(k - 2):
-                n_exit(k - 2)
+            if ok(k - 3):
+                n_exit(k - 3)
             if ok(k):
                 stt(k, [0])
                 a_tr(k, 0)
@@ -310,18 +310,18 @@ def tile_relationalgraphconvolution_pa_t_kernel(tc, node_features, relation_feat
                 bank_t = psum.tile([P, P], BF16, tag="R", bufs=2)
                 nc.tensor.transpose(bank_t[:], relz[:], identb[:])
                 nc.vector.tensor_copy(out=relcol[:], in_=bank_t[:, 0:NB * NR])
-            if ok(k - 1):
-                r_tr(k - 1)
+            if ok(k - 2):
+                r_tr(k - 2)
             if k == 3:
                 wb_quant(0)
             if k == 5:
                 wb_quant(1)
             if k % 4 == 0 and 1 <= k // 4 < NB:
                 quant_nf(k // 4)
-            if ok(k - 1):
-                q_a(k - 1)
             if ok(k - 2):
-                q_s(k - 2)
+                q_a(k - 2)
+            if ok(k - 4):
+                q_s(k - 4)
             if ok(k):
                 a_exit(k, 0)
             if k == 0:
@@ -339,17 +339,17 @@ def tile_relationalgraphconvolution_pa_t_kernel(tc, node_features, relation_feat
                 wb_tr(k - 1)
             if ok(k - LD):
                 d_exit(k - LD)
-            if ok(k - 1) and k - 1 > 0:
-                r_mm(k - 1)
-            if ok(k - 1):
-                b_mm(k - 1)
-            elif k == 0:
+            if ok(k - 2) and k - 2 > 0:
+                r_mm(k - 2)
+            if ok(k - 2):
+                b_mm(k - 2)
+            elif k < 2:
                 dummy(2)
             if ok(k):
                 stt(k, [1, 2] if k > 0 else [1, 2, 3])
                 a_exit(k, 1)
-            if ok(k - 1):
-                rel_exit(k - 1)
+            if ok(k - 2):
+                rel_exit(k - 2)
             if 1 <= k < 5:
                 wb_exit(k - 1)
             if k % 4 == 3 and 1 <= (k + 1) // 4 < NB:

@@ -65,11 +65,6 @@ def tile_relationalgraphconvolution_pa_t_kernel(tc, node_features, relation_feat
         wbc = const.tile([P, 1024], U32, name="wbc", align_bytes=64)
         wbs = const.tile([P, 1024], U8, name="wbs", align_bytes=64)
 
-        zc = const.tile([P, 512], U32, name="zc", align_bytes=64)
-        zs = const.tile([P, 512], U8, name="zs", align_bytes=64)
-        zb = const.tile([P, 2048], BF16, name="zb", align_bytes=64)
-        nc.vector.memset(zb[:].bitcast(I32), 0)
-        nc.vector.quantize_mx(out=zc[:].bitcast(FP8X4), scales=zs[:], in_=zb[:])
         nc.vector.memset(relz[:], 0.0)
         ones = const.tile([P, P], BF16, name="ones")
         nc.vector.memset(ones[:], 1.0)
@@ -148,19 +143,6 @@ def tile_relationalgraphconvolution_pa_t_kernel(tc, node_features, relation_feat
                 out=gw[:, h * 512:(h + 1) * 512].rearrange("p (rr i u) -> p rr i u", rr=2, u=2),
                 in_=st["A"][(u, h)][:].rearrange("p (rr u i) -> p rr i u", rr=2, u=2),
             )
-
-        def dummy(n):
-            for i in range(n):
-                bank_x = psum.tile([P, 512], F32, tag="X", bufs=1)
-                nc.tensor.matmul_mx(
-                    out=bank_x[:],
-                    lhsT=zc[:, 0:128].bitcast(FP8X4),
-                    lhsT_scale=zs[:, 0:128],
-                    rhs=zc[:].bitcast(FP8X4),
-                    rhs_scale=zs[:],
-                    start=True,
-                    stop=True,
-                )
 
         def nf_regroup(b):
             nc.scalar.copy(
@@ -296,7 +278,6 @@ def tile_relationalgraphconvolution_pa_t_kernel(tc, node_features, relation_feat
         def ok(u):
             return 0 <= u < NU
 
-        dummy(4)
 
         for k in range(NU + LD + 1):
             if k < 24:
@@ -331,8 +312,6 @@ def tile_relationalgraphconvolution_pa_t_kernel(tc, node_features, relation_feat
                 )
             if ok(k - LD):
                 d_mm(k - LD)
-            elif k < LD:
-                dummy(2)
             if ok(k):
                 a_tr(k, 1)
             if 1 <= k < 5:
@@ -343,8 +322,6 @@ def tile_relationalgraphconvolution_pa_t_kernel(tc, node_features, relation_feat
                 r_mm(k - 2)
             if ok(k - 2):
                 b_mm(k - 2)
-            elif k < 2:
-                dummy(2)
             if ok(k):
                 stt(k, [1, 2] if k > 0 else [1, 2, 3])
                 a_exit(k, 1)

@@ -23,7 +23,7 @@ NT = 4
 NU = NB * NT
 LD = 5
 MANUAL = True
-V_D1_FROM = 27
+V_D1_FROM = 31
 
 
 def tile_relationalgraphconvolution_pa_t_kernel(tc, node_features, relation_features, adj, Wb, out):
@@ -44,6 +44,12 @@ def tile_relationalgraphconvolution_pa_t_kernel(tc, node_features, relation_feat
             nc.sync.dma_start(
                 out=adj_sb[b][:].rearrange("p (r t j) -> p r t j", r=NR, t=NT)[:, :, it, :],
                 in_=adj[b].rearrange("r (p t) j -> p r t j", t=NT)[:, :, it, :],
+            )
+
+        def load_it_half(b, it, h):
+            nc.sync.dma_start(
+                out=adj_sb[b][:].rearrange("p (r t j) -> p r t j", r=NR, t=NT)[:, 2 * h:2 * h + 2, it, :],
+                in_=adj[b].rearrange("r (p t) j -> p r t j", t=NT)[:, 2 * h:2 * h + 2, it, :],
             )
 
         def load_r(b, r):
@@ -68,7 +74,8 @@ def tile_relationalgraphconvolution_pa_t_kernel(tc, node_features, relation_feat
         nc.vector.memset(relz[:], 0.0)
         ones = const.tile([P, P], BF16, name="ones")
         nc.vector.memset(ones[:], 1.0)
-        load_it(0, 0)
+        load_it_half(0, 0, 0)
+        load_it_half(0, 0, 1)
         nc.sync.dma_start(
             out=nfraw[:, 0:256].rearrange("q (u x) -> q u x", u=2),
             in_=node_features[0].rearrange("(u q e) d -> q u (e d)", u=2, e=2),
@@ -123,7 +130,7 @@ def tile_relationalgraphconvolution_pa_t_kernel(tc, node_features, relation_feat
         def a_tr(u, h):
             b, it = divmod(u, NT)
             adjw = adj_sb[b][:].bitcast(F32)
-            bank_a = psum.tile([P, 512], F32, tag="A", bufs=2)
+            bank_a = psum.tile([P, 512], F32, tag="A", bufs=3)
             for rr in range(2):
                 for uu in range(2):
                     col = ((2 * h + rr) * NT + it) * 256 + 128 * uu
@@ -293,7 +300,7 @@ def tile_relationalgraphconvolution_pa_t_kernel(tc, node_features, relation_feat
                 nc.vector.tensor_copy(out=relcol[:], in_=bank_t[:, 0:NB * NR])
             if ok(k - 2):
                 r_tr(k - 2)
-            if k == 3:
+            if k == 4:
                 wb_quant(0)
             if k == 5:
                 wb_quant(1)

@@ -11,19 +11,16 @@ BF16 = mybir.dt.bfloat16
 F32 = mybir.dt.float32
 U32 = mybir.dt.uint32
 U8 = mybir.dt.uint8
-I32 = mybir.dt.int32
 FP8X4 = mybir.dt.float8_e4m3fn_x4
 MULT = mybir.AluOpType.mult
-ADD = mybir.AluOpType.add
 
 P = 128
 NB = 8
 NR = 4
 NT = 4
 NU = NB * NT
-LD = 5
-MANUAL = True
-V_D1_FROM = 31
+LAG = 5
+NS = 24
 
 
 def tile_relationalgraphconvolution_pa_t_kernel(tc, node_features, relation_features, adj, Wb, out):
@@ -32,25 +29,29 @@ def tile_relationalgraphconvolution_pa_t_kernel(tc, node_features, relation_feat
         const = ctx.enter_context(tc.tile_pool(name="const", bufs=1))
         work = ctx.enter_context(tc.tile_pool(name="work", bufs=2))
         psum = ctx.enter_context(tc.psum_pool(name="psum", bufs=1))
-        if MANUAL:
-            ctx.enter_context(tc.manual_schedule())
+        ctx.enter_context(tc.manual_schedule())
 
-        adj_sb = []
-        for b in range(NB):
+        adj_0 = []
+        for it in range(NT):
+            adj_i = const.tile([P, NR * 512], BF16, name="adj0_%d" % it)
+            adj_0.append(adj_i)
+        adj_sb = [None]
+        for b in range(1, NB):
             adj_t = const.tile([P, NR * NT * 512], BF16, name="adj%d" % b)
             adj_sb.append(adj_t)
 
-        def load_it(b, it):
+        def load_it(it, r0, r1):
             nc.sync.dma_start(
-                out=adj_sb[b][:].rearrange("p (r t j) -> p r t j", r=NR, t=NT)[:, :, it, :],
-                in_=adj[b].rearrange("r (p t) j -> p r t j", t=NT)[:, :, it, :],
+                out=adj_0[it][:].rearrange("p (r j) -> p r j", r=NR)[:, r0:r1, :],
+                in_=adj[0].rearrange("r (p t) j -> p r t j", t=NT)[:, r0:r1, it, :],
             )
 
-        def load_it_half(b, it, h):
-            nc.sync.dma_start(
-                out=adj_sb[b][:].rearrange("p (r t j) -> p r t j", r=NR, t=NT)[:, 2 * h:2 * h + 2, it, :],
-                in_=adj[b].rearrange("r (p t) j -> p r t j", t=NT)[:, 2 * h:2 * h + 2, it, :],
-            )
+        def words(u, r, uu):
+            b, it = divmod(u, NT)
+            if b == 0:
+                return adj_0[it][:].bitcast(F32)[:, r * 256 + 128 * uu:r * 256 + 128 * uu + 128]
+            col = (r * NT + it) * 256 + 128 * uu
+            return adj_sb[b][:].bitcast(F32)[:, col:col + 128]
 
         def load_r(b, r):
             nc.sync.dma_start(
@@ -60,101 +61,75 @@ def tile_relationalgraphconvolution_pa_t_kernel(tc, node_features, relation_feat
 
         nfraw = const.tile([P, 2048], BF16, name="nfraw")
         nfg = const.tile([P, 2048], BF16, name="nfg", align_bytes=64)
-        nfc = const.tile([P, NB * 128], U32, name="nfc", align_bytes=64)
-        nfs = const.tile([P, NB * 128], U8, name="nfs", align_bytes=64)
-        relz = const.tile([P, P], BF16, name="relz")
-        relcol = const.tile([P, NB * NR], F32, name="relcol")
+        nfc = const.tile([P, NB * 64], U32, name="nfc", align_bytes=64)
+        nfs = const.tile([P, NB * 64], U8, name="nfs", align_bytes=64)
+        relb = const.tile([P, NB * NR * 64], BF16, name="relb")
         identf = const.tile([P, P], F32, name="identf")
-        identb = const.tile([P, P], BF16, name="identb")
+        ones = const.tile([P, NS], BF16, name="ones")
         wb_sb = const.tile([P, 4096], BF16, name="wb_sb")
         wbg = const.tile([P, 4096], BF16, name="wbg", align_bytes=64)
         wbc = const.tile([P, 1024], U32, name="wbc", align_bytes=64)
         wbs = const.tile([P, 1024], U8, name="wbs", align_bytes=64)
 
-        nc.vector.memset(relz[:], 0.0)
-        ones = const.tile([P, P], BF16, name="ones")
         nc.vector.memset(ones[:], 1.0)
-        load_it_half(0, 0, 0)
-        load_it_half(0, 0, 1)
+        load_it(0, 0, 2)
+        load_it(0, 2, 4)
         nc.sync.dma_start(
             out=nfraw[:, 0:256].rearrange("q (u x) -> q u x", u=2),
             in_=node_features[0].rearrange("(u q e) d -> q u (e d)", u=2, e=2),
         )
-        nc.sync.dma_start(out=relz[0:32, 64:128], in_=relation_features.rearrange("b r f -> (b r) f"))
-        load_it(0, 1)
+        load_it(1, 0, 4)
+        relrow = relation_features.rearrange("b r f -> (b r f)")
+        nc.sync.dma_start(out=relb[:, 0:256], in_=relrow[0:256].partition_broadcast(P))
         wb_view = Wb.rearrange("(t p) k -> p t k", p=P)
         nc.sync.dma_start(out=wb_sb[:, 0:2048].rearrange("p (t k) -> p t k", t=4), in_=wb_view[:, 0:4, :])
-        load_it(0, 2)
+        load_it(2, 0, 4)
         nc.sync.dma_start(out=wb_sb[:, 2048:4096].rearrange("p (t k) -> p t k", t=4), in_=wb_view[:, 4:8, :])
-        load_it(0, 3)
+        load_it(3, 0, 4)
         nc.sync.dma_start(
             out=nfraw[:, 256:2048].rearrange("q (c x) -> q c x", c=14),
             in_=node_features[1:8].rearrange("b (u q e) d -> q (b u) (e d)", u=2, e=2),
         )
-        for it in range(NT):
-            load_it(1, it)
+        for r in range(NR):
+            load_r(1, r)
+        nc.sync.dma_start(out=relb[:, 256:2048], in_=relrow[256:2048].partition_broadcast(P))
 
         make_identity(nc, identf[:])
-        make_identity(nc, identb[:])
-        nc.vector.memset(nfc[:].bitcast(I32), 0)
-        nc.vector.memset(nfs[:].bitcast(I32), 0)
+
+        def nf_regroup(b, copy):
+            copy(
+                out=nfg[:, b * 256:(b + 1) * 256].rearrange("q (d t) -> q d t", t=4),
+                in_=nfraw[:, b * 256:(b + 1) * 256].rearrange("q (t d) -> q d t", t=4),
+            )
 
         def quant_nf(b):
             nc.vector.quantize_mx(
-                out=nfc[:, b * 128:b * 128 + 64].bitcast(FP8X4),
-                scales=nfs[:, b * 128:b * 128 + 64],
+                out=nfc[:, b * 64:(b + 1) * 64].bitcast(FP8X4),
+                scales=nfs[:, b * 64:(b + 1) * 64],
                 in_=nfg[:, b * 256:(b + 1) * 256],
             )
 
-        st = {"rs": {}, "A": {}, "grp": {}, "cA": {}, "sA": {}, "N": {}, "R": {}, "g2": {}, "c2": {}, "s2": {}, "D": {}}
-
-        def stt(u, rlist):
-            b, it = divmod(u, NT)
-            if u not in st["rs"]:
-                rs = work.tile([P, NR], F32, tag="rs", bufs=4)
-                st["rs"][u] = rs
-            rs = st["rs"][u]
-            for r in rlist:
-                base = (r * NT + it) * 512
-                junk = work.tile([P, 256], F32, tag="junk", bufs=2)
-                nc.vector.scalar_tensor_tensor(
-                    out=junk[:],
-                    in0=adj_sb[b][:, base:base + 256],
-                    scalar=1.0,
-                    in1=adj_sb[b][:, base + 256:base + 512],
-                    op0=MULT,
-                    op1=ADD,
-                    accum_out=rs[:, r:r + 1],
-                )
+        st = {"A": {}, "grp": {}, "cA": {}, "sA": {}, "N": {}, "RS": {}, "sup": {}, "S": {}, "g2": {}, "c2": {}, "s2": {}, "D": {}}
 
         def a_tr(u, h):
-            b, it = divmod(u, NT)
-            adjw = adj_sb[b][:].bitcast(F32)
             bank_a = psum.tile([P, 512], F32, tag="A", bufs=3)
             for rr in range(2):
                 for uu in range(2):
-                    col = ((2 * h + rr) * NT + it) * 256 + 128 * uu
                     nc.tensor.transpose(
                         bank_a[:, (rr * 2 + uu) * 128:(rr * 2 + uu + 1) * 128],
-                        adjw[:, col:col + 128],
+                        words(u, 2 * h + rr, uu),
                         identf[:],
                     )
             st["A"][(u, h)] = bank_a
 
         def a_exit(u, h):
             if u not in st["grp"]:
-                grp = work.tile([P, 2048], BF16, tag="grp", bufs=4, align_bytes=64)
+                grp = work.tile([P, 2048], BF16, tag="grp", bufs=3, align_bytes=64)
                 st["grp"][u] = grp
             gw = st["grp"][u][:].bitcast(F32)
             nc.scalar.copy(
                 out=gw[:, h * 512:(h + 1) * 512].rearrange("p (rr i u) -> p rr i u", rr=2, u=2),
                 in_=st["A"][(u, h)][:].rearrange("p (rr u i) -> p rr i u", rr=2, u=2),
-            )
-
-        def nf_regroup(b):
-            nc.scalar.copy(
-                out=nfg[:, b * 256:(b + 1) * 256].rearrange("q (d t) -> q d t", t=4),
-                in_=nfraw[:, b * 256:(b + 1) * 256].rearrange("q (t d) -> q d t", t=4),
             )
 
         def q_a(u):
@@ -164,68 +139,78 @@ def tile_relationalgraphconvolution_pa_t_kernel(tc, node_features, relation_feat
             st["sA"][u] = s_a
             nc.vector.quantize_mx(out=c_a[:].bitcast(FP8X4), scales=s_a[:], in_=st["grp"][u][:])
 
+        def rs_mm(u):
+            bank_rs = psum.tile([P, NR * NS], F32, tag="RS", bufs=1)
+            st["RS"][u] = bank_rs
+            gv = st["grp"][u][:].rearrange("p (r i t) -> p r i t", r=NR, t=4)
+            for r in range(NR):
+                for t in range(4):
+                    nc.tensor.matmul(
+                        out=bank_rs[:, r * NS:(r + 1) * NS],
+                        lhsT=gv[:, r, :, t],
+                        rhs=ones[:],
+                        start=(t == 0),
+                        stop=(t == 3),
+                    )
+
         def b_mm(u):
             b, it = divmod(u, NT)
-            bank_n = psum.tile([P, 512], F32, tag="N", bufs=1)
+            bank_n = psum.tile([P, 256], F32, tag="N", bufs=1)
             st["N"][u] = bank_n
-            nc.tensor.matmul_mx(
-                out=bank_n[:],
-                lhsT=nfc[:, b * 128:(b + 1) * 128].bitcast(FP8X4),
-                lhsT_scale=nfs[:, b * 128:(b + 1) * 128],
-                rhs=st["cA"][u][:].bitcast(FP8X4),
-                rhs_scale=st["sA"][u][:],
-                start=True,
-                stop=True,
-            )
-
-        def r_tr(u):
-            bank_r = psum.tile([P, 512], F32, tag="R", bufs=2)
-            st["R"][u] = bank_r
-            rs = st["rs"][u]
-            for r in range(NR if u == 0 else NR - 1):
-                nc.tensor.transpose(
-                    bank_r[:, r * 128:(r + 1) * 128],
-                    rs[:, r:r + 1].to_broadcast([P, P]),
-                    identf[:],
+            for r in range(NR):
+                nc.tensor.matmul_mx(
+                    out=bank_n[:, r * 64:(r + 1) * 64],
+                    lhsT=st["cA"][u][:, r * 128:(r + 1) * 128].bitcast(FP8X4),
+                    lhsT_scale=st["sA"][u][:, r * 128:(r + 1) * 128],
+                    rhs=nfc[:, b * 64:(b + 1) * 64].bitcast(FP8X4),
+                    rhs_scale=nfs[:, b * 64:(b + 1) * 64],
+                    start=True,
+                    stop=True,
                 )
 
-        def r_mm(u):
-            gv = st["grp"][u][:].rearrange("p (r i t) -> p r i t", r=NR, t=4)
-            for t in range(4):
-                nc.tensor.matmul(
-                    out=st["R"][u][:, 384:512],
-                    lhsT=ones[:],
-                    rhs=gv[:, 3, :, t],
-                    start=(t == 0),
-                    stop=(t == 3),
-                )
-
-        def get_g2(u):
-            if u not in st["g2"]:
-                g2 = work.tile([P, 512], BF16, tag="g2", bufs=4, align_bytes=64)
-                st["g2"][u] = g2
-            return st["g2"][u]
+        def get_sup(u):
+            if u not in st["sup"]:
+                sup = work.tile([P, 512], BF16, tag="sup", bufs=3, align_bytes=64)
+                st["sup"][u] = sup
+            return st["sup"][u][:].rearrange("p (r x) -> p r x", r=NR)
 
         def n_exit(u):
-            g2 = get_g2(u)
             nc.scalar.copy(
-                out=g2[0:64, :].rearrange("p (i r) -> p i r", r=NR),
-                in_=st["N"][u][0:64, :].rearrange("p (r i) -> p i r", r=NR),
+                out=get_sup(u)[:, :, 0:64],
+                in_=st["N"][u][:].rearrange("p (r d) -> p r d", r=NR),
             )
 
-        def rel_exit(u):
+        def rel(u):
             b, it = divmod(u, NT)
-            g2 = get_g2(u)
             nc.vector.tensor_tensor(
-                out=g2[:].rearrange("p (i r) -> p i r", r=NR),
-                in0=st["R"][u][:].rearrange("p (r i) -> p i r", r=NR),
-                in1=relcol[:, NR * b:NR * (b + 1)].unsqueeze(1).to_broadcast([P, P, NR]),
+                out=get_sup(u)[:, :, 64:128],
+                in0=relb[:, b * 256:(b + 1) * 256].rearrange("p (r f) -> p r f", r=NR),
+                in1=st["RS"][u][:].rearrange("p (r n) -> p r n", r=NR)[:, :, 0:1].to_broadcast([P, NR, 64]),
                 op=MULT,
             )
 
+        def s_tr(u):
+            bank_s = psum.tile([P, 256], F32, tag="S", bufs=1)
+            st["S"][u] = bank_s
+            supw = st["sup"][u][:].bitcast(F32)
+            for uu in range(2):
+                nc.tensor.transpose(
+                    bank_s[:, uu * 128:(uu + 1) * 128],
+                    supw[:, uu * 128:(uu + 1) * 128],
+                    identf[:],
+                )
+
+        def s_exit(u):
+            g2 = work.tile([P, 512], BF16, tag="g2", bufs=3, align_bytes=64)
+            st["g2"][u] = g2
+            nc.vector.tensor_copy(
+                out=g2[:].bitcast(F32).rearrange("p (i u) -> p i u", u=2),
+                in_=st["S"][u][:].rearrange("p (u i) -> p i u", u=2),
+            )
+
         def q_s(u):
-            c_2 = work.tile([P, P], U32, tag="c2", bufs=LD + 2, align_bytes=64)
-            s_2 = work.tile([P, P], U8, tag="s2", bufs=LD + 2, align_bytes=64)
+            c_2 = work.tile([P, P], U32, tag="c2", bufs=3, align_bytes=64)
+            s_2 = work.tile([P, P], U8, tag="s2", bufs=3, align_bytes=64)
             st["c2"][u] = c_2
             st["s2"][u] = s_2
             nc.vector.quantize_mx(out=c_2[:].bitcast(FP8X4), scales=s_2[:], in_=st["g2"][u][:])
@@ -244,35 +229,38 @@ def tile_relationalgraphconvolution_pa_t_kernel(tc, node_features, relation_feat
                     stop=True,
                 )
                 banks.append(bank_d)
-            st["D"][u] = banks
+            ost = work.tile([P, 1024], F32, tag="ost", bufs=6)
+            st["D"][u] = (banks, ost)
 
-        def d_exit(u):
+        def d_exit_0(u):
+            banks, ost = st["D"][u]
+            nc.scalar.copy(out=ost[:, 0:512], in_=banks[0][:])
+
+        def d_exit_1(u):
             b, it = divmod(u, NT)
-            ost = work.tile([P, 1024], F32, tag="ost", bufs=4)
-            nc.scalar.copy(out=ost[:, 0:512], in_=st["D"][u][0][:])
-            if u >= V_D1_FROM:
-                nc.vector.tensor_copy(out=ost[:, 512:1024], in_=st["D"][u][1][:])
-            else:
-                nc.scalar.copy(out=ost[:, 512:1024], in_=st["D"][u][1][:])
+            banks, ost = st["D"][u]
+            nc.vector.tensor_copy(out=ost[:, 512:1024], in_=banks[1][:])
             nc.sync.dma_start(out=out[b].rearrange("(p t) n -> p t n", t=NT)[:, it, :], in_=ost[:])
 
         wbank = {}
 
         def wb_tr(g):
-            bank_w = psum.tile([P, 1024], BF16, tag="D", bufs=2)
+            bank_w = psum.tile([P, 512], F32, tag="D", bufs=2)
             wbank[g] = bank_w
+            wbw = wb_sb[:].bitcast(F32)
             for nn in range(2):
-                for t in range(4):
+                for uu in range(2):
+                    col = (2 * g + nn) * 256 + uu * 128
                     nc.tensor.transpose(
-                        bank_w[:, (nn * 4 + t) * 128:(nn * 4 + t + 1) * 128],
-                        wb_sb[:, (2 * g + nn) * 512 + t * 128:(2 * g + nn) * 512 + (t + 1) * 128],
-                        identb[:],
+                        bank_w[:, (nn * 2 + uu) * 128:(nn * 2 + uu + 1) * 128],
+                        wbw[:, col:col + 128],
+                        identf[:],
                     )
 
-        def wb_exit(g):
-            nc.scalar.copy(
-                out=wbg[:, g * 1024:(g + 1) * 1024].rearrange("p (nn n t) -> p nn n t", nn=2, t=4),
-                in_=wbank[g][:].rearrange("p (nn t n) -> p nn n t", nn=2, t=4),
+        def wb_exit(g, copy):
+            copy(
+                out=wbg[:, g * 1024:(g + 1) * 1024].bitcast(F32).rearrange("p (nn n u) -> p nn n u", nn=2, u=2),
+                in_=wbank[g][:].rearrange("p (nn u n) -> p nn n u", nn=2, u=2),
             )
 
         def wb_quant(h):
@@ -285,58 +273,50 @@ def tile_relationalgraphconvolution_pa_t_kernel(tc, node_features, relation_feat
         def ok(u):
             return 0 <= u < NU
 
-
-        for k in range(NU + LD + 1):
-            if k < 24:
-                load_r(2 + k // 4, k % 4)
-            if ok(k - 3):
-                n_exit(k - 3)
+        for k in range(NU + LAG):
+            if k < 12:
+                for j in (2 * k, 2 * k + 1):
+                    load_r(2 + j // 4, j % 4)
             if ok(k):
-                stt(k, [0])
                 a_tr(k, 0)
-            if k == 1:
-                bank_t = psum.tile([P, P], BF16, tag="R", bufs=2)
-                nc.tensor.transpose(bank_t[:], relz[:], identb[:])
-                nc.vector.tensor_copy(out=relcol[:], in_=bank_t[:, 0:NB * NR])
+                a_tr(k, 1)
+            if ok(k - 3):
+                s_tr(k - 3)
+            if k in (1, 2):
+                wb_tr(2 * k - 2)
+                wb_tr(2 * k - 1)
+            if ok(k - 5):
+                d_exit_0(k - 5)
             if ok(k - 2):
-                r_tr(k - 2)
-            if k == 4:
-                wb_quant(0)
-            if k == 5:
-                wb_quant(1)
-            if k % 4 == 0 and 1 <= k // 4 < NB:
-                quant_nf(k // 4)
-            if ok(k - 2):
-                q_a(k - 2)
-            if ok(k - 4):
-                q_s(k - 4)
+                n_exit(k - 2)
             if ok(k):
                 a_exit(k, 0)
-            if k == 0:
-                nc.vector.tensor_copy(
-                    out=nfg[:, 0:256].rearrange("q (d t) -> q d t", t=4),
-                    in_=nfraw[:, 0:256].rearrange("q (t d) -> q d t", t=4),
-                )
-            if ok(k - LD):
-                d_mm(k - LD)
-            if ok(k):
-                a_tr(k, 1)
-            if 1 <= k < 5:
-                wb_tr(k - 1)
-            if ok(k - LD):
-                d_exit(k - LD)
-            if ok(k - 2) and k - 2 > 0:
-                r_mm(k - 2)
-            if ok(k - 2):
-                b_mm(k - 2)
-            if ok(k):
-                stt(k, [1, 2] if k > 0 else [1, 2, 3])
                 a_exit(k, 1)
-            if ok(k - 2):
-                rel_exit(k - 2)
-            if 1 <= k < 5:
-                wb_exit(k - 1)
-            if k % 4 == 3 and 1 <= (k + 1) // 4 < NB:
-                nf_regroup((k + 1) // 4)
             if k == 0:
-                quant_nf(0)
+                nf_regroup(0, nc.vector.tensor_copy)
+            if k % 4 == 3 and 1 <= (k + 1) // 4 < NB:
+                nf_regroup((k + 1) // 4, nc.vector.tensor_copy)
+            if ok(k - 2):
+                rel(k - 2)
+            if ok(k - 4):
+                q_s(k - 4)
+            if k == 3:
+                wb_quant(0)
+                wb_quant(1)
+            if ok(k - 5):
+                d_exit_1(k - 5)
+            if k % 4 == 0 and k // 4 < NB:
+                quant_nf(k // 4)
+            if ok(k - 1):
+                q_a(k - 1)
+            if ok(k - 3):
+                s_exit(k - 3)
+            if k in (1, 2):
+                wb_exit(2 * k - 2, nc.vector.tensor_copy)
+                wb_exit(2 * k - 1, nc.vector.tensor_copy)
+            if ok(k - 1):
+                rs_mm(k - 1)
+            if ok(k - 4):
+                d_mm(k - 4)
+            if ok(k - 1):
+                b_mm(k - 1)

@@ -13,6 +13,7 @@ U32 = mybir.dt.uint32
 U8 = mybir.dt.uint8
 FP8X4 = mybir.dt.float8_e4m3fn_x4
 MULT = mybir.AluOpType.mult
+ADD = mybir.AluOpType.add
 
 P = 128
 NB = 8
@@ -20,6 +21,7 @@ NR = 4
 NT = 4
 NU = NB * NT
 LAG = 5
+RV = 2
 NS = 24
 
 
@@ -46,12 +48,12 @@ def tile_relationalgraphconvolution_pa_t_kernel(tc, node_features, relation_feat
                 in_=adj[0].rearrange("r (p t) j -> p r t j", t=NT)[:, r0:r1, it, :],
             )
 
-        def words(u, r, uu):
+        def rows(u, r):
             b, it = divmod(u, NT)
             if b == 0:
-                return adj_0[it][:].bitcast(F32)[:, r * 256 + 128 * uu:r * 256 + 128 * uu + 128]
-            col = (r * NT + it) * 256 + 128 * uu
-            return adj_sb[b][:].bitcast(F32)[:, col:col + 128]
+                return adj_0[it][:, r * 512:(r + 1) * 512]
+            col = (r * NT + it) * 512
+            return adj_sb[b][:, col:col + 512]
 
         def load_r(b, r):
             nc.sync.dma_start(
@@ -109,7 +111,7 @@ def tile_relationalgraphconvolution_pa_t_kernel(tc, node_features, relation_feat
                 in_=nfg[:, b * 256:(b + 1) * 256],
             )
 
-        st = {"A": {}, "grp": {}, "cA": {}, "sA": {}, "N": {}, "RS": {}, "sup": {}, "S": {}, "g2": {}, "c2": {}, "s2": {}, "D": {}}
+        st = {"A": {}, "grp": {}, "cA": {}, "sA": {}, "N": {}, "RS": {}, "sup": {}, "S": {}, "g2": {}, "c2": {}, "s2": {}, "D": {}, "rs": {}}
 
         def a_tr(u, h):
             bank_a = psum.tile([P, 512], F32, tag="A", bufs=3)
@@ -117,7 +119,7 @@ def tile_relationalgraphconvolution_pa_t_kernel(tc, node_features, relation_feat
                 for uu in range(2):
                     nc.tensor.transpose(
                         bank_a[:, (rr * 2 + uu) * 128:(rr * 2 + uu + 1) * 128],
-                        words(u, 2 * h + rr, uu),
+                        rows(u, 2 * h + rr).bitcast(F32)[:, 128 * uu:128 * (uu + 1)],
                         identf[:],
                     )
             st["A"][(u, h)] = bank_a
@@ -139,14 +141,29 @@ def tile_relationalgraphconvolution_pa_t_kernel(tc, node_features, relation_feat
             st["sA"][u] = s_a
             nc.vector.quantize_mx(out=c_a[:].bitcast(FP8X4), scales=s_a[:], in_=st["grp"][u][:])
 
+        def rs_vec(u):
+            rs = work.tile([P, RV], F32, tag="rs", bufs=4)
+            st["rs"][u] = rs
+            for r in range(RV):
+                junk = work.tile([P, 256], F32, tag="junk", bufs=2)
+                nc.vector.scalar_tensor_tensor(
+                    out=junk[:],
+                    in0=rows(u, r)[:, 0:256],
+                    scalar=1.0,
+                    in1=rows(u, r)[:, 256:512],
+                    op0=MULT,
+                    op1=ADD,
+                    accum_out=rs[:, r:r + 1],
+                )
+
         def rs_mm(u):
-            bank_rs = psum.tile([P, NR * NS], F32, tag="RS", bufs=1)
+            bank_rs = psum.tile([P, (NR - RV) * NS], F32, tag="RS", bufs=1)
             st["RS"][u] = bank_rs
             gv = st["grp"][u][:].rearrange("p (r i t) -> p r i t", r=NR, t=4)
-            for r in range(NR):
+            for r in range(RV, NR):
                 for t in range(4):
                     nc.tensor.matmul(
-                        out=bank_rs[:, r * NS:(r + 1) * NS],
+                        out=bank_rs[:, (r - RV) * NS:(r - RV + 1) * NS],
                         lhsT=gv[:, r, :, t],
                         rhs=ones[:],
                         start=(t == 0),
@@ -182,10 +199,17 @@ def tile_relationalgraphconvolution_pa_t_kernel(tc, node_features, relation_feat
 
         def rel(u):
             b, it = divmod(u, NT)
+            relv = relb[:, b * 256:(b + 1) * 256].rearrange("p (r f) -> p r f", r=NR)
             nc.vector.tensor_tensor(
-                out=get_sup(u)[:, :, 64:128],
-                in0=relb[:, b * 256:(b + 1) * 256].rearrange("p (r f) -> p r f", r=NR),
-                in1=st["RS"][u][:].rearrange("p (r n) -> p r n", r=NR)[:, :, 0:1].to_broadcast([P, NR, 64]),
+                out=get_sup(u)[:, 0:RV, 64:128],
+                in0=relv[:, 0:RV, :],
+                in1=st["rs"][u][:].unsqueeze(2).to_broadcast([P, RV, 64]),
+                op=MULT,
+            )
+            nc.vector.tensor_tensor(
+                out=get_sup(u)[:, RV:NR, 64:128],
+                in0=relv[:, RV:NR, :],
+                in1=st["RS"][u][:].rearrange("p (r n) -> p r n", r=NR - RV)[:, :, 0:1].to_broadcast([P, NR - RV, 64]),
                 op=MULT,
             )
 
@@ -203,7 +227,7 @@ def tile_relationalgraphconvolution_pa_t_kernel(tc, node_features, relation_feat
         def s_exit(u):
             g2 = work.tile([P, 512], BF16, tag="g2", bufs=3, align_bytes=64)
             st["g2"][u] = g2
-            nc.vector.tensor_copy(
+            nc.scalar.copy(
                 out=g2[:].bitcast(F32).rearrange("p (i u) -> p i u", u=2),
                 in_=st["S"][u][:].rearrange("p (u i) -> p i u", u=2),
             )
@@ -229,7 +253,7 @@ def tile_relationalgraphconvolution_pa_t_kernel(tc, node_features, relation_feat
                     stop=True,
                 )
                 banks.append(bank_d)
-            ost = work.tile([P, 1024], F32, tag="ost", bufs=6)
+            ost = work.tile([P, 1024], F32, tag="ost", bufs=10)
             st["D"][u] = (banks, ost)
 
         def d_exit_0(u):
@@ -292,6 +316,8 @@ def tile_relationalgraphconvolution_pa_t_kernel(tc, node_features, relation_feat
             if ok(k):
                 a_exit(k, 0)
                 a_exit(k, 1)
+            if ok(k - 3):
+                s_exit(k - 3)
             if k == 0:
                 nf_regroup(0, nc.vector.tensor_copy)
             if k % 4 == 3 and 1 <= (k + 1) // 4 < NB:
@@ -309,8 +335,8 @@ def tile_relationalgraphconvolution_pa_t_kernel(tc, node_features, relation_feat
                 quant_nf(k // 4)
             if ok(k - 1):
                 q_a(k - 1)
-            if ok(k - 3):
-                s_exit(k - 3)
+            if ok(k):
+                rs_vec(k)
             if k in (1, 2):
                 wb_exit(2 * k - 2, nc.vector.tensor_copy)
                 wb_exit(2 * k - 1, nc.vector.tensor_copy)

@@ -21,7 +21,7 @@ NR = 4
 NT = 4
 NU = NB * NT
 LAG = 5
-RV = 2
+RV = 1
 NS = 24
 
 

@@ -21,7 +21,9 @@ NR = 4
 NT = 4
 NU = NB * NT
 LAG = 5
-RV = 1
+NE = 2
+UE = NE * NT
+VEC = ((0,), (0, 1))
 NS = 24
 
 
@@ -33,25 +35,26 @@ def tile_relationalgraphconvolution_pa_t_kernel(tc, node_features, relation_feat
         psum = ctx.enter_context(tc.psum_pool(name="psum", bufs=1))
         ctx.enter_context(tc.manual_schedule())
 
-        adj_0 = []
-        for it in range(NT):
-            adj_i = const.tile([P, NR * 512], BF16, name="adj0_%d" % it)
-            adj_0.append(adj_i)
-        adj_sb = [None]
-        for b in range(1, NB):
+        adj_u = []
+        for u in range(UE):
+            adj_i = const.tile([P, NR * 512], BF16, name="adju%d" % u)
+            adj_u.append(adj_i)
+        adj_sb = [None] * NE
+        for b in range(NE, NB):
             adj_t = const.tile([P, NR * NT * 512], BF16, name="adj%d" % b)
             adj_sb.append(adj_t)
 
-        def load_it(it, r0, r1):
+        def load_u(u, r0, r1):
+            b, it = divmod(u, NT)
             nc.sync.dma_start(
-                out=adj_0[it][:].rearrange("p (r j) -> p r j", r=NR)[:, r0:r1, :],
-                in_=adj[0].rearrange("r (p t) j -> p r t j", t=NT)[:, r0:r1, it, :],
+                out=adj_u[u][:].rearrange("p (r j) -> p r j", r=NR)[:, r0:r1, :],
+                in_=adj[b].rearrange("r (p t) j -> p r t j", t=NT)[:, r0:r1, it, :],
             )
 
         def rows(u, r):
             b, it = divmod(u, NT)
-            if b == 0:
-                return adj_0[it][:, r * 512:(r + 1) * 512]
+            if u < UE:
+                return adj_u[u][:, r * 512:(r + 1) * 512]
             col = (r * NT + it) * 512
             return adj_sb[b][:, col:col + 512]
 
@@ -74,27 +77,36 @@ def tile_relationalgraphconvolution_pa_t_kernel(tc, node_features, relation_feat
         wbs = const.tile([P, 1024], U8, name="wbs", align_bytes=64)
 
         nc.vector.memset(ones[:], 1.0)
-        load_it(0, 0, 2)
-        load_it(0, 2, 4)
+        relrow = relation_features.rearrange("b r f -> (b r f)")
+        wb_view = Wb.rearrange("(t p) k -> p t k", p=P)
+
+        def load_wb(h):
+            nc.sync.dma_start(
+                out=wb_sb[:, h * 2048:(h + 1) * 2048].rearrange("p (t k) -> p t k", t=4),
+                in_=wb_view[:, 4 * h:4 * h + 4, :],
+            )
+
+        load_u(0, 0, 2)
+        load_u(0, 2, 4)
         nc.sync.dma_start(
             out=nfraw[:, 0:256].rearrange("q (u x) -> q u x", u=2),
             in_=node_features[0].rearrange("(u q e) d -> q u (e d)", u=2, e=2),
         )
-        load_it(1, 0, 4)
-        relrow = relation_features.rearrange("b r f -> (b r f)")
+        load_u(1, 0, 4)
         nc.sync.dma_start(out=relb[:, 0:256], in_=relrow[0:256].partition_broadcast(P))
-        wb_view = Wb.rearrange("(t p) k -> p t k", p=P)
-        nc.sync.dma_start(out=wb_sb[:, 0:2048].rearrange("p (t k) -> p t k", t=4), in_=wb_view[:, 0:4, :])
-        load_it(2, 0, 4)
-        nc.sync.dma_start(out=wb_sb[:, 2048:4096].rearrange("p (t k) -> p t k", t=4), in_=wb_view[:, 4:8, :])
-        load_it(3, 0, 4)
+        load_u(2, 0, 4)
+        load_wb(0)
+        load_u(3, 0, 4)
+        load_wb(1)
+        load_u(4, 0, 4)
         nc.sync.dma_start(
             out=nfraw[:, 256:2048].rearrange("q (c x) -> q c x", c=14),
             in_=node_features[1:8].rearrange("b (u q e) d -> q (b u) (e d)", u=2, e=2),
         )
-        for r in range(NR):
-            load_r(1, r)
+        load_u(5, 0, 4)
         nc.sync.dma_start(out=relb[:, 256:2048], in_=relrow[256:2048].partition_broadcast(P))
+        load_u(6, 0, 4)
+        load_u(7, 0, 4)
 
         make_identity(nc, identf[:])
 
@@ -141,10 +153,18 @@ def tile_relationalgraphconvolution_pa_t_kernel(tc, node_features, relation_feat
             st["sA"][u] = s_a
             nc.vector.quantize_mx(out=c_a[:].bitcast(FP8X4), scales=s_a[:], in_=st["grp"][u][:])
 
+        def n_sb(u):
+            return len(VEC[u % 2])
+
+        def get_rs(u):
+            if u not in st["rs"]:
+                rs = work.tile([P, NR], F32, tag="rs", bufs=5)
+                st["rs"][u] = rs
+            return st["rs"][u]
+
         def rs_vec(u):
-            rs = work.tile([P, RV], F32, tag="rs", bufs=4)
-            st["rs"][u] = rs
-            for r in range(RV):
+            rs = get_rs(u)
+            for r in VEC[u % 2]:
                 junk = work.tile([P, 256], F32, tag="junk", bufs=2)
                 nc.vector.scalar_tensor_tensor(
                     out=junk[:],
@@ -157,13 +177,14 @@ def tile_relationalgraphconvolution_pa_t_kernel(tc, node_features, relation_feat
                 )
 
         def rs_mm(u):
-            bank_rs = psum.tile([P, (NR - RV) * NS], F32, tag="RS", bufs=1)
+            RV = n_sb(u)
+            bank_rs = psum.tile([P, NR * NS], F32, tag="RS", bufs=1)
             st["RS"][u] = bank_rs
             gv = st["grp"][u][:].rearrange("p (r i t) -> p r i t", r=NR, t=4)
             for r in range(RV, NR):
                 for t in range(4):
                     nc.tensor.matmul(
-                        out=bank_rs[:, (r - RV) * NS:(r - RV + 1) * NS],
+                        out=bank_rs[:, r * NS:(r + 1) * NS],
                         lhsT=gv[:, r, :, t],
                         rhs=ones[:],
                         start=(t == 0),
@@ -199,17 +220,19 @@ def tile_relationalgraphconvolution_pa_t_kernel(tc, node_features, relation_feat
 
         def rel(u):
             b, it = divmod(u, NT)
+            RV = n_sb(u)
             relv = relb[:, b * 256:(b + 1) * 256].rearrange("p (r f) -> p r f", r=NR)
-            nc.vector.tensor_tensor(
-                out=get_sup(u)[:, 0:RV, 64:128],
-                in0=relv[:, 0:RV, :],
-                in1=st["rs"][u][:].unsqueeze(2).to_broadcast([P, RV, 64]),
-                op=MULT,
-            )
+            for r in range(RV):
+                nc.scalar.activation(
+                    out=get_sup(u)[:, r, 64:128],
+                    in_=relv[:, r, :],
+                    func=mybir.ActivationFunctionType.Copy,
+                    scale=st["rs"][u][:, r:r + 1],
+                )
             nc.vector.tensor_tensor(
                 out=get_sup(u)[:, RV:NR, 64:128],
                 in0=relv[:, RV:NR, :],
-                in1=st["RS"][u][:].rearrange("p (r n) -> p r n", r=NR - RV)[:, :, 0:1].to_broadcast([P, NR - RV, 64]),
+                in1=st["RS"][u][:].rearrange("p (r n) -> p r n", r=NR)[:, RV:NR, 0:1].to_broadcast([P, NR - RV, 64]),
                 op=MULT,
             )
 
@@ -256,15 +279,16 @@ def tile_relationalgraphconvolution_pa_t_kernel(tc, node_features, relation_feat
             ost = work.tile([P, 1024], F32, tag="ost", bufs=10)
             st["D"][u] = (banks, ost)
 
-        def d_exit_0(u):
-            banks, ost = st["D"][u]
-            nc.scalar.copy(out=ost[:, 0:512], in_=banks[0][:])
-
-        def d_exit_1(u):
+        def d_exit(u, h):
             b, it = divmod(u, NT)
             banks, ost = st["D"][u]
-            nc.vector.tensor_copy(out=ost[:, 512:1024], in_=banks[1][:])
-            nc.sync.dma_start(out=out[b].rearrange("(p t) n -> p t n", t=NT)[:, it, :], in_=ost[:])
+            copy = nc.vector.tensor_copy if h else nc.scalar.copy
+            copy(out=ost[:, h * 512:(h + 1) * 512], in_=banks[h][:])
+            dst = out[b].rearrange("(p t) n -> p t n", t=NT)[:, it, :]
+            if u == NU - 1:
+                nc.sync.dma_start(out=dst[:, h * 512:(h + 1) * 512], in_=ost[:, h * 512:(h + 1) * 512])
+            elif h == 1:
+                nc.sync.dma_start(out=dst, in_=ost[:])
 
         wbank = {}
 
@@ -297,21 +321,25 @@ def tile_relationalgraphconvolution_pa_t_kernel(tc, node_features, relation_feat
         def ok(u):
             return 0 <= u < NU
 
+
         for k in range(NU + LAG):
             if k < 12:
                 for j in (2 * k, 2 * k + 1):
                     load_r(2 + j // 4, j % 4)
+
             if ok(k):
                 a_tr(k, 0)
                 a_tr(k, 1)
             if ok(k - 3):
                 s_tr(k - 3)
-            if k in (1, 2):
-                wb_tr(2 * k - 2)
-                wb_tr(2 * k - 1)
+            if k in (2, 3):
+                wb_tr(2 * k - 4)
+                wb_tr(2 * k - 3)
+            if ok(k - 2) and k >= NU:
+                n_exit(k - 2)
             if ok(k - 5):
-                d_exit_0(k - 5)
-            if ok(k - 2):
+                d_exit(k - 5, 0)
+            if ok(k - 2) and k < NU:
                 n_exit(k - 2)
             if ok(k):
                 a_exit(k, 0)
@@ -320,29 +348,33 @@ def tile_relationalgraphconvolution_pa_t_kernel(tc, node_features, relation_feat
                 s_exit(k - 3)
             if k == 0:
                 nf_regroup(0, nc.vector.tensor_copy)
-            if k % 4 == 3 and 1 <= (k + 1) // 4 < NB:
-                nf_regroup((k + 1) // 4, nc.vector.tensor_copy)
+                quant_nf(0)
+            if k % 4 == 1 and 1 <= k // 4 < NB:
+                quant_nf(k // 4)
+            if ok(k - 1) and k >= NU:
+                q_a(k - 1)
             if ok(k - 2):
                 rel(k - 2)
             if ok(k - 4):
                 q_s(k - 4)
-            if k == 3:
-                wb_quant(0)
-                wb_quant(1)
+            if k in (3, 4):
+                wb_quant(k - 3)
             if ok(k - 5):
-                d_exit_1(k - 5)
-            if k % 4 == 0 and k // 4 < NB:
-                quant_nf(k // 4)
-            if ok(k - 1):
+                d_exit(k - 5, 1)
+            if ok(k - 1) and k < NU:
                 q_a(k - 1)
             if ok(k):
                 rs_vec(k)
-            if k in (1, 2):
-                wb_exit(2 * k - 2, nc.vector.tensor_copy)
-                wb_exit(2 * k - 1, nc.vector.tensor_copy)
+            if k % 4 == 0 and 1 <= k // 4 < NB:
+                nf_regroup(k // 4, nc.vector.tensor_copy)
+            if k in (2, 3):
+                wb_exit(2 * k - 4, nc.vector.tensor_copy)
+                wb_exit(2 * k - 3, nc.scalar.copy)
             if ok(k - 1):
                 rs_mm(k - 1)
+            if ok(k - 1) and k >= NU:
+                b_mm(k - 1)
             if ok(k - 4):
                 d_mm(k - 4)
-            if ok(k - 1):
+            if ok(k - 1) and k < NU:
                 b_mm(k - 1)

@@ -86,26 +86,29 @@ def tile_relationalgraphconvolution_pa_t_kernel(tc, node_features, relation_feat
                 in_=wb_view[:, 4 * h:4 * h + 4, :],
             )
 
+        def load_nf(b0, b1):
+            nc.sync.dma_start(
+                out=nfraw[:, b0 * 256:b1 * 256].rearrange("q (c x) -> q c x", c=2 * (b1 - b0)),
+                in_=node_features[b0:b1].rearrange("b (u q e) d -> q (b u) (e d)", u=2, e=2),
+            )
+
+        def load_rel(b0, b1):
+            nc.sync.dma_start(out=relb[:, b0 * 256:b1 * 256], in_=relrow[b0 * 256:b1 * 256].partition_broadcast(P))
+
         load_u(0, 0, 2)
         load_u(0, 2, 4)
-        nc.sync.dma_start(
-            out=nfraw[:, 0:256].rearrange("q (u x) -> q u x", u=2),
-            in_=node_features[0].rearrange("(u q e) d -> q u (e d)", u=2, e=2),
-        )
+        load_nf(0, 2)
         load_u(1, 0, 4)
-        nc.sync.dma_start(out=relb[:, 0:256], in_=relrow[0:256].partition_broadcast(P))
+        load_rel(0, 2)
         load_u(2, 0, 4)
         load_wb(0)
         load_u(3, 0, 4)
         load_wb(1)
         load_u(4, 0, 4)
-        nc.sync.dma_start(
-            out=nfraw[:, 256:2048].rearrange("q (c x) -> q c x", c=14),
-            in_=node_features[1:8].rearrange("b (u q e) d -> q (b u) (e d)", u=2, e=2),
-        )
         load_u(5, 0, 4)
-        nc.sync.dma_start(out=relb[:, 256:2048], in_=relrow[256:2048].partition_broadcast(P))
         load_u(6, 0, 4)
+        load_nf(2, 3)
+        load_rel(2, 3)
         load_u(7, 0, 4)
 
         make_identity(nc, identf[:])
@@ -223,11 +226,13 @@ def tile_relationalgraphconvolution_pa_t_kernel(tc, node_features, relation_feat
             RV = n_sb(u)
             relv = relb[:, b * 256:(b + 1) * 256].rearrange("p (r f) -> p r f", r=NR)
             for r in range(RV):
-                nc.scalar.activation(
+                nc.gpsimd.tensor_scalar(
                     out=get_sup(u)[:, r, 64:128],
-                    in_=relv[:, r, :],
-                    func=mybir.ActivationFunctionType.Copy,
-                    scale=st["rs"][u][:, r:r + 1],
+                    in0=relv[:, r, :],
+                    scalar1=st["rs"][u][:, r:r + 1],
+                    scalar2=0.0,
+                    op0=MULT,
+                    op1=ADD,
                 )
             nc.vector.tensor_tensor(
                 out=get_sup(u)[:, RV:NR, 64:128],
@@ -323,9 +328,11 @@ def tile_relationalgraphconvolution_pa_t_kernel(tc, node_features, relation_feat
 
 
         for k in range(NU + LAG):
-            if k < 12:
-                for j in (2 * k, 2 * k + 1):
-                    load_r(2 + j // 4, j % 4)
+            if k < 4 * (NB - NE):
+                load_r(NE + k // 4, k % 4)
+            if k == 4:
+                load_nf(3, NB)
+                load_rel(3, NB)
 
             if ok(k):
                 a_tr(k, 0)

@@ -168,12 +168,12 @@ def tile_relationalgraphconvolution_pa_t_kernel(tc, node_features, relation_feat
         def rs_vec(u):
             rs = get_rs(u)
             for r in VEC[u % 2]:
-                junk = work.tile([P, 256], F32, tag="junk", bufs=2)
-                nc.vector.scalar_tensor_tensor(
+                junk = work.tile([P, 512], BF16, tag="junk", bufs=2)
+                nc.vector.tensor_scalar(
                     out=junk[:],
-                    in0=rows(u, r)[:, 0:256],
-                    scalar=1.0,
-                    in1=rows(u, r)[:, 256:512],
+                    in0=rows(u, r),
+                    scalar1=1.0,
+                    scalar2=0.0,
                     op0=MULT,
                     op1=ADD,
                     accum_out=rs[:, r:r + 1],

@@ -23,7 +23,7 @@ NU = NB * NT
 LAG = 5
 NE = 2
 UE = NE * NT
-VEC = ((0,), (0, 1))
+VEC = ((0, 1), (0, 1))
 NS = 24
 
 

@@ -23,8 +23,8 @@ NU = NB * NT
 LAG = 5
 NE = 2
 UE = NE * NT
-VEC = ((0, 1), (0, 1))
-NS = 24
+TREL = (0, 2)
+VREL = (1, 3)
 
 
 def tile_relationalgraphconvolution_pa_t_kernel(tc, node_features, relation_features, adj, Wb, out):
@@ -70,13 +70,11 @@ def tile_relationalgraphconvolution_pa_t_kernel(tc, node_features, relation_feat
         nfs = const.tile([P, NB * 64], U8, name="nfs", align_bytes=64)
         relb = const.tile([P, NB * NR * 64], BF16, name="relb")
         identf = const.tile([P, P], F32, name="identf")
-        ones = const.tile([P, NS], BF16, name="ones")
         wb_sb = const.tile([P, 4096], BF16, name="wb_sb")
         wbg = const.tile([P, 4096], BF16, name="wbg", align_bytes=64)
         wbc = const.tile([P, 1024], U32, name="wbc", align_bytes=64)
         wbs = const.tile([P, 1024], U8, name="wbs", align_bytes=64)
 
-        nc.vector.memset(ones[:], 1.0)
         relrow = relation_features.rearrange("b r f -> (b r f)")
         wb_view = Wb.rearrange("(t p) k -> p t k", p=P)
 
@@ -126,7 +124,7 @@ def tile_relationalgraphconvolution_pa_t_kernel(tc, node_features, relation_feat
                 in_=nfg[:, b * 256:(b + 1) * 256],
             )
 
-        st = {"A": {}, "grp": {}, "cA": {}, "sA": {}, "N": {}, "RS": {}, "sup": {}, "S": {}, "g2": {}, "c2": {}, "s2": {}, "D": {}, "rs": {}}
+        st = {"A": {}, "grp": {}, "cA": {}, "sA": {}, "N": {}, "sup": {}, "S": {}, "g2": {}, "c2": {}, "s2": {}, "D": {}, "rs": {}}
 
         def a_tr(u, h):
             bank_a = psum.tile([P, 512], F32, tag="A", bufs=3)
@@ -156,9 +154,6 @@ def tile_relationalgraphconvolution_pa_t_kernel(tc, node_features, relation_feat
             st["sA"][u] = s_a
             nc.vector.quantize_mx(out=c_a[:].bitcast(FP8X4), scales=s_a[:], in_=st["grp"][u][:])
 
-        def n_sb(u):
-            return len(VEC[u % 2])
-
         def get_rs(u):
             if u not in st["rs"]:
                 rs = work.tile([P, NR], F32, tag="rs", bufs=5)
@@ -167,7 +162,7 @@ def tile_relationalgraphconvolution_pa_t_kernel(tc, node_features, relation_feat
 
         def rs_vec(u):
             rs = get_rs(u)
-            for r in VEC[u % 2]:
+            for r in VREL:
                 junk = work.tile([P, 512], BF16, tag="junk", bufs=2)
                 nc.vector.tensor_scalar(
                     out=junk[:],
@@ -180,27 +175,26 @@ def tile_relationalgraphconvolution_pa_t_kernel(tc, node_features, relation_feat
                 )
 
         def rs_mm(u):
-            RV = n_sb(u)
-            bank_rs = psum.tile([P, NR * NS], F32, tag="RS", bufs=1)
-            st["RS"][u] = bank_rs
+            b = u // NT
+            bank_n = psum.tile([P, 384], F32, tag="N", bufs=2)
+            st["N"][u] = bank_n
             gv = st["grp"][u][:].rearrange("p (r i t) -> p r i t", r=NR, t=4)
-            for r in range(RV, NR):
+            for r in TREL:
                 for t in range(4):
                     nc.tensor.matmul(
-                        out=bank_rs[:, r * NS:(r + 1) * NS],
+                        out=bank_n[:, r * 96 + 64:r * 96 + 128],
                         lhsT=gv[:, r, :, t],
-                        rhs=ones[:],
+                        rhs=relb[:, (b * NR + r) * 64:(b * NR + r + 1) * 64],
                         start=(t == 0),
                         stop=(t == 3),
                     )
 
         def b_mm(u):
             b, it = divmod(u, NT)
-            bank_n = psum.tile([P, 256], F32, tag="N", bufs=1)
-            st["N"][u] = bank_n
+            bank_n = st["N"][u]
             for r in range(NR):
                 nc.tensor.matmul_mx(
-                    out=bank_n[:, r * 64:(r + 1) * 64],
+                    out=bank_n[:, (r // 2) * 192 + (r % 2) * 128:(r // 2) * 192 + (r % 2) * 128 + 64],
                     lhsT=st["cA"][u][:, r * 128:(r + 1) * 128].bitcast(FP8X4),
                     lhsT_scale=st["sA"][u][:, r * 128:(r + 1) * 128],
                     rhs=nfc[:, b * 64:(b + 1) * 64].bitcast(FP8X4),
@@ -213,33 +207,25 @@ def tile_relationalgraphconvolution_pa_t_kernel(tc, node_features, relation_feat
             if u not in st["sup"]:
                 sup = work.tile([P, 512], BF16, tag="sup", bufs=3, align_bytes=64)
                 st["sup"][u] = sup
-            return st["sup"][u][:].rearrange("p (r x) -> p r x", r=NR)
+            return st["sup"][u][:].rearrange("p (h x) -> p h x", h=2)
 
         def n_exit(u):
             nc.scalar.copy(
-                out=get_sup(u)[:, :, 0:64],
-                in_=st["N"][u][:].rearrange("p (r d) -> p r d", r=NR),
+                out=get_sup(u)[:, :, 0:192],
+                in_=st["N"][u][:].rearrange("p (h x) -> p h x", h=2),
             )
 
         def rel(u):
-            b, it = divmod(u, NT)
-            RV = n_sb(u)
-            relv = relb[:, b * 256:(b + 1) * 256].rearrange("p (r f) -> p r f", r=NR)
-            for r in range(RV):
+            b = u // NT
+            for h, r in enumerate(VREL):
                 nc.gpsimd.tensor_scalar(
-                    out=get_sup(u)[:, r, 64:128],
-                    in0=relv[:, r, :],
+                    out=get_sup(u)[:, h, 192:256],
+                    in0=relb[:, (b * NR + r) * 64:(b * NR + r + 1) * 64],
                     scalar1=st["rs"][u][:, r:r + 1],
                     scalar2=0.0,
                     op0=MULT,
                     op1=ADD,
                 )
-            nc.vector.tensor_tensor(
-                out=get_sup(u)[:, RV:NR, 64:128],
-                in0=relv[:, RV:NR, :],
-                in1=st["RS"][u][:].rearrange("p (r n) -> p r n", r=NR)[:, RV:NR, 0:1].to_broadcast([P, NR - RV, 64]),
-                op=MULT,
-            )
 
         def s_tr(u):
             bank_s = psum.tile([P, 256], F32, tag="S", bufs=1)

@@ -111,11 +111,13 @@ def tile_relationalgraphconvolution_pa_t_kernel(tc, node_features, relation_feat
 
         make_identity(nc, identf[:])
 
-        def nf_regroup(b, copy):
-            copy(
-                out=nfg[:, b * 256:(b + 1) * 256].rearrange("q (d t) -> q d t", t=4),
-                in_=nfraw[:, b * 256:(b + 1) * 256].rearrange("q (t d) -> q d t", t=4),
-            )
+        def nf_regroup(b):
+            dst = nfg[:, b * 256:(b + 1) * 256].rearrange("q (d t) -> q d t", t=4)
+            src = nfraw[:, b * 256:(b + 1) * 256].rearrange("q (t d) -> q d t", t=4)
+            if b == 0:
+                nc.vector.tensor_copy(out=dst, in_=src)
+            else:
+                nc.gpsimd.tensor_scalar(out=dst, in0=src, scalar1=1.0, scalar2=0.0, op0=MULT, op1=ADD)
 
         def quant_nf(b):
             nc.vector.quantize_mx(
@@ -340,7 +342,7 @@ def tile_relationalgraphconvolution_pa_t_kernel(tc, node_features, relation_feat
             if ok(k - 3):
                 s_exit(k - 3)
             if k == 0:
-                nf_regroup(0, nc.vector.tensor_copy)
+                nf_regroup(0)
                 quant_nf(0)
             if k % 4 == 1 and 1 <= k // 4 < NB:
                 quant_nf(k // 4)
@@ -359,7 +361,7 @@ def tile_relationalgraphconvolution_pa_t_kernel(tc, node_features, relation_feat
             if ok(k):
                 rs_vec(k)
             if k % 4 == 0 and 1 <= k // 4 < NB:
-                nf_regroup(k // 4, nc.vector.tensor_copy)
+                nf_regroup(k // 4)
             if k in (2, 3):
                 wb_exit(2 * k - 4, nc.vector.tensor_copy)
                 wb_exit(2 * k - 3, nc.scalar.copy)

@@ -23,8 +23,9 @@ NU = NB * NT
 LAG = 5
 NE = 2
 UE = NE * NT
-TREL = (0, 2)
-VREL = (1, 3)
+TREL = (0, 1)
+VREL = (2, 3)
+NS = 32
 
 
 def tile_relationalgraphconvolution_pa_t_kernel(tc, node_features, relation_features, adj, Wb, out):
@@ -70,11 +71,13 @@ def tile_relationalgraphconvolution_pa_t_kernel(tc, node_features, relation_feat
         nfs = const.tile([P, NB * 64], U8, name="nfs", align_bytes=64)
         relb = const.tile([P, NB * NR * 64], BF16, name="relb")
         identf = const.tile([P, P], F32, name="identf")
+        ones = const.tile([P, NS], BF16, name="ones")
         wb_sb = const.tile([P, 4096], BF16, name="wb_sb")
         wbg = const.tile([P, 4096], BF16, name="wbg", align_bytes=64)
         wbc = const.tile([P, 1024], U32, name="wbc", align_bytes=64)
         wbs = const.tile([P, 1024], U8, name="wbs", align_bytes=64)
 
+        nc.vector.memset(ones[:], 1.0)
         relrow = relation_features.rearrange("b r f -> (b r f)")
         wb_view = Wb.rearrange("(t p) k -> p t k", p=P)
 
@@ -177,16 +180,15 @@ def tile_relationalgraphconvolution_pa_t_kernel(tc, node_features, relation_feat
                 )
 
         def rs_mm(u):
-            b = u // NT
-            bank_n = psum.tile([P, 384], F32, tag="N", bufs=2)
+            bank_n = psum.tile([P, 256 + len(TREL) * NS], F32, tag="N", bufs=2)
             st["N"][u] = bank_n
             gv = st["grp"][u][:].rearrange("p (r i t) -> p r i t", r=NR, t=4)
             for r in TREL:
                 for t in range(4):
                     nc.tensor.matmul(
-                        out=bank_n[:, r * 96 + 64:r * 96 + 128],
+                        out=bank_n[:, 256 + r * NS:256 + (r + 1) * NS],
                         lhsT=gv[:, r, :, t],
-                        rhs=relb[:, (b * NR + r) * 64:(b * NR + r + 1) * 64],
+                        rhs=ones[:],
                         start=(t == 0),
                         stop=(t == 3),
                     )
@@ -196,7 +198,7 @@ def tile_relationalgraphconvolution_pa_t_kernel(tc, node_features, relation_feat
             bank_n = st["N"][u]
             for r in range(NR):
                 nc.tensor.matmul_mx(
-                    out=bank_n[:, (r // 2) * 192 + (r % 2) * 128:(r // 2) * 192 + (r % 2) * 128 + 64],
+                    out=bank_n[:, r * 64:(r + 1) * 64],
                     lhsT=st["cA"][u][:, r * 128:(r + 1) * 128].bitcast(FP8X4),
                     lhsT_scale=st["sA"][u][:, r * 128:(r + 1) * 128],
                     rhs=nfc[:, b * 64:(b + 1) * 64].bitcast(FP8X4),
@@ -209,25 +211,28 @@ def tile_relationalgraphconvolution_pa_t_kernel(tc, node_features, relation_feat
             if u not in st["sup"]:
                 sup = work.tile([P, 512], BF16, tag="sup", bufs=3, align_bytes=64)
                 st["sup"][u] = sup
-            return st["sup"][u][:].rearrange("p (h x) -> p h x", h=2)
+            return st["sup"][u][:].rearrange("p (r x) -> p r x", r=NR)
 
         def n_exit(u):
             nc.scalar.copy(
-                out=get_sup(u)[:, :, 0:192],
-                in_=st["N"][u][:].rearrange("p (h x) -> p h x", h=2),
+                out=get_sup(u)[:, :, 0:64],
+                in_=st["N"][u][:, 0:256].rearrange("p (r d) -> p r d", r=NR),
+            )
+
+        def rs_exit(u):
+            nc.scalar.copy(
+                out=get_rs(u)[:, 0:len(TREL)],
+                in_=st["N"][u][:, 256:256 + len(TREL) * NS].rearrange("p (r n) -> p r n", n=NS)[:, :, 0],
             )
 
         def rel(u):
             b = u // NT
-            for h, r in enumerate(VREL):
-                nc.gpsimd.tensor_scalar(
-                    out=get_sup(u)[:, h, 192:256],
-                    in0=relb[:, (b * NR + r) * 64:(b * NR + r + 1) * 64],
-                    scalar1=st["rs"][u][:, r:r + 1],
-                    scalar2=0.0,
-                    op0=MULT,
-                    op1=ADD,
-                )
+            nc.gpsimd.tensor_tensor(
+                out=get_sup(u)[:, :, 64:128],
+                in0=relb[:, b * 256:(b + 1) * 256].rearrange("p (r f) -> p r f", r=NR),
+                in1=st["rs"][u][:].rearrange("p (r n) -> p r n", n=1).to_broadcast([P, NR, 64]),
+                op=MULT,
+            )
 
         def s_tr(u):
             bank_s = psum.tile([P, 256], F32, tag="S", bufs=1)
@@ -321,55 +326,52 @@ def tile_relationalgraphconvolution_pa_t_kernel(tc, node_features, relation_feat
             if k == 4:
                 load_nf(3, NB)
                 load_rel(3, NB)
-
             if ok(k):
                 a_tr(k, 0)
+            if ok(k):
                 a_tr(k, 1)
             if ok(k - 3):
                 s_tr(k - 3)
             if k in (2, 3):
-                wb_tr(2 * k - 4)
-                wb_tr(2 * k - 3)
-            if ok(k - 2) and k >= NU:
-                n_exit(k - 2)
-            if ok(k - 5):
-                d_exit(k - 5, 0)
-            if ok(k - 2) and k < NU:
-                n_exit(k - 2)
-            if ok(k):
-                a_exit(k, 0)
-                a_exit(k, 1)
-            if ok(k - 3):
-                s_exit(k - 3)
+                wb_tr(2 * (k - 2))
+                wb_tr(2 * (k - 2) + 1)
             if k == 0:
                 nf_regroup(0)
                 quant_nf(0)
-            if k % 4 == 1 and 1 <= k // 4 < NB:
+            if k % 4 == 0 and 1 <= k // 4 < NB:
                 quant_nf(k // 4)
-            if ok(k - 1) and k >= NU:
-                q_a(k - 1)
+            if ok(k - 5):
+                d_exit(k - 5, 0)
+            if ok(k - 2):
+                rs_exit(k - 2)
+            if ok(k - 2):
+                n_exit(k - 2)
+            if ok(k):
+                a_exit(k, 0)
+            if ok(k):
+                a_exit(k, 1)
+            if ok(k - 3):
+                s_exit(k - 3)
             if ok(k - 2):
                 rel(k - 2)
+            if ok(k - 1):
+                q_a(k - 1)
             if ok(k - 4):
                 q_s(k - 4)
             if k in (3, 4):
                 wb_quant(k - 3)
             if ok(k - 5):
                 d_exit(k - 5, 1)
-            if ok(k - 1) and k < NU:
-                q_a(k - 1)
             if ok(k):
                 rs_vec(k)
-            if k % 4 == 0 and 1 <= k // 4 < NB:
-                nf_regroup(k // 4)
-            if k in (2, 3):
-                wb_exit(2 * k - 4, nc.vector.tensor_copy)
-                wb_exit(2 * k - 3, nc.scalar.copy)
             if ok(k - 1):
                 rs_mm(k - 1)
-            if ok(k - 1) and k >= NU:
-                b_mm(k - 1)
             if ok(k - 4):
                 d_mm(k - 4)
-            if ok(k - 1) and k < NU:
+            if ok(k - 1):
                 b_mm(k - 1)
+            if k % 4 == 2 and k // 4 + 1 < NB:
+                nf_regroup(k // 4 + 1)
+            if k in (2, 3):
+                wb_exit(2 * (k - 2), nc.vector.tensor_copy)
+                wb_exit(2 * (k - 2) + 1, nc.scalar.copy)

@@ -79,12 +79,12 @@ def tile_relationalgraphconvolution_pa_t_kernel(tc, node_features, relation_feat
 
         nc.vector.memset(ones[:], 1.0)
         relrow = relation_features.rearrange("b r f -> (b r f)")
-        wb_view = Wb.rearrange("(t p) k -> p t k", p=P)
+        wb_view = Wb.rearrange("(g p s) k -> p g (s k)", p=P, s=4)
 
         def load_wb(h):
             nc.sync.dma_start(
-                out=wb_sb[:, h * 2048:(h + 1) * 2048].rearrange("p (t k) -> p t k", t=4),
-                in_=wb_view[:, 4 * h:4 * h + 4, :],
+                out=wb_sb[:, h * 2048:(h + 1) * 2048],
+                in_=wb_view[:, h, :],
             )
 
         def load_nf(b0, b1):
@@ -98,19 +98,20 @@ def tile_relationalgraphconvolution_pa_t_kernel(tc, node_features, relation_feat
 
         load_u(0, 0, 2)
         load_u(0, 2, 4)
-        load_nf(0, 2)
+        load_nf(0, 1)
         load_u(1, 0, 4)
         load_rel(0, 2)
         load_u(2, 0, 4)
         load_wb(0)
         load_u(3, 0, 4)
         load_wb(1)
+        load_nf(1, 2)
         load_u(4, 0, 4)
         load_u(5, 0, 4)
         load_u(6, 0, 4)
+        load_u(7, 0, 4)
         load_nf(2, 3)
         load_rel(2, 3)
-        load_u(7, 0, 4)
 
         make_identity(nc, identf[:])
 
@@ -263,7 +264,10 @@ def tile_relationalgraphconvolution_pa_t_kernel(tc, node_features, relation_feat
         def d_mm(u):
             banks = []
             for h in range(2):
-                bank_d = psum.tile([P, 512], F32, tag="D", bufs=2)
+                if u >= NU - 4 and u % 2 == 0:
+                    bank_d = psum.tile([P, 512], F32, tag="A", bufs=3)
+                else:
+                    bank_d = psum.tile([P, 512], F32, tag="D", bufs=2)
                 nc.tensor.matmul_mx(
                     out=bank_d[:],
                     lhsT=st["c2"][u][:].bitcast(FP8X4),
@@ -304,9 +308,11 @@ def tile_relationalgraphconvolution_pa_t_kernel(tc, node_features, relation_feat
                     )
 
         def wb_exit(g, copy):
+            h, j = divmod(g, 2)
+            wide = wbg[:, h * 2048:(h + 1) * 2048].bitcast(F32).rearrange("p (n s u) -> p n s u", s=4, u=2)
             copy(
-                out=wbg[:, g * 1024:(g + 1) * 1024].bitcast(F32).rearrange("p (nn n u) -> p nn n u", nn=2, u=2),
-                in_=wbank[g][:].rearrange("p (nn u n) -> p nn n u", nn=2, u=2),
+                out=wide[:, :, 2 * j:2 * j + 2, :],
+                in_=wbank[g][:].rearrange("p (s u n) -> p n s u", s=2, u=2),
             )
 
         def wb_quant(h):
@@ -373,5 +379,5 @@ def tile_relationalgraphconvolution_pa_t_kernel(tc, node_features, relation_feat
             if k % 4 == 2 and k // 4 + 1 < NB:
                 nf_regroup(k // 4 + 1)
             if k in (2, 3):
-                wb_exit(2 * (k - 2), nc.vector.tensor_copy)
+                wb_exit(2 * (k - 2), nc.scalar.copy)
                 wb_exit(2 * (k - 2) + 1, nc.scalar.copy)

@@ -23,8 +23,6 @@ NU = NB * NT
 LAG = 5
 NE = 2
 UE = NE * NT
-TREL = (0, 1)
-VREL = (2, 3)
 NS = 32
 
 
@@ -132,6 +130,9 @@ def tile_relationalgraphconvolution_pa_t_kernel(tc, node_features, relation_feat
 
         st = {"A": {}, "grp": {}, "cA": {}, "sA": {}, "N": {}, "sup": {}, "S": {}, "g2": {}, "c2": {}, "s2": {}, "D": {}, "rs": {}}
 
+        def n_t(u):
+            return 1 if u % 6 == 4 else 2
+
         def a_tr(u, h):
             bank_a = psum.tile([P, 512], F32, tag="A", bufs=3)
             for rr in range(2):
@@ -168,7 +169,7 @@ def tile_relationalgraphconvolution_pa_t_kernel(tc, node_features, relation_feat
 
         def rs_vec(u):
             rs = get_rs(u)
-            for r in VREL:
+            for r in range(n_t(u), NR):
                 junk = work.tile([P, 512], BF16, tag="junk", bufs=2)
                 nc.vector.tensor_scalar(
                     out=junk[:],
@@ -181,10 +182,10 @@ def tile_relationalgraphconvolution_pa_t_kernel(tc, node_features, relation_feat
                 )
 
         def rs_mm(u):
-            bank_n = psum.tile([P, 256 + len(TREL) * NS], F32, tag="N", bufs=2)
+            bank_n = psum.tile([P, 256 + 2 * NS], F32, tag="N", bufs=2)
             st["N"][u] = bank_n
             gv = st["grp"][u][:].rearrange("p (r i t) -> p r i t", r=NR, t=4)
-            for r in TREL:
+            for r in range(n_t(u)):
                 for t in range(4):
                     nc.tensor.matmul(
                         out=bank_n[:, 256 + r * NS:256 + (r + 1) * NS],
@@ -222,8 +223,8 @@ def tile_relationalgraphconvolution_pa_t_kernel(tc, node_features, relation_feat
 
         def rs_exit(u):
             nc.scalar.copy(
-                out=get_rs(u)[:, 0:len(TREL)],
-                in_=st["N"][u][:, 256:256 + len(TREL) * NS].rearrange("p (r n) -> p r n", n=NS)[:, :, 0],
+                out=get_rs(u)[:, 0:n_t(u)],
+                in_=st["N"][u][:, 256:256 + n_t(u) * NS].rearrange("p (r n) -> p r n", n=NS)[:, :, 0],
             )
 
         def rel(u):

from contextlib import ExitStack

import concourse.bass as bass
import concourse.mybir as mybir
import concourse.tile as tile
from concourse.masks import make_identity

FLOPS = 2 * 8 * 4 * 512 * 512 * 64 + 2 * 8 * 512 * 512 * 1024

BF16 = mybir.dt.bfloat16
F32 = mybir.dt.float32
U32 = mybir.dt.uint32
U8 = mybir.dt.uint8
FP8X4 = mybir.dt.float8_e4m3fn_x4
MULT = mybir.AluOpType.mult
ADD = mybir.AluOpType.add

P = 128
NB = 8
NR = 4
NT = 4
NU = NB * NT
LAG = 5
NE = 2
UE = NE * NT
NS = 32


def tile_relationalgraphconvolution_pa_t_kernel(tc, node_features, relation_features, adj, Wb, out):
    nc = tc.nc
    with ExitStack() as ctx:
        const = ctx.enter_context(tc.tile_pool(name="const", bufs=1))
        work = ctx.enter_context(tc.tile_pool(name="work", bufs=2))
        psum = ctx.enter_context(tc.psum_pool(name="psum", bufs=1))
        ctx.enter_context(tc.manual_schedule())

        adj_u = []
        for u in range(UE):
            adj_i = const.tile([P, NR * 512], BF16, name="adju%d" % u)
            adj_u.append(adj_i)
        adj_sb = [None] * NE
        for b in range(NE, NB):
            adj_t = const.tile([P, NR * NT * 512], BF16, name="adj%d" % b)
            adj_sb.append(adj_t)

        def load_u(u, r0, r1):
            b, it = divmod(u, NT)
            nc.sync.dma_start(
                out=adj_u[u][:].rearrange("p (r j) -> p r j", r=NR)[:, r0:r1, :],
                in_=adj[b].rearrange("r (p t) j -> p r t j", t=NT)[:, r0:r1, it, :],
            )

        def rows(u, r):
            b, it = divmod(u, NT)
            if u < UE:
                return adj_u[u][:, r * 512:(r + 1) * 512]
            col = (r * NT + it) * 512
            return adj_sb[b][:, col:col + 512]

        def load_r(b, r):
            nc.sync.dma_start(
                out=adj_sb[b][:, r * 2048:(r + 1) * 2048],
                in_=adj[b, r].rearrange("(p t) j -> p (t j)", t=NT),
            )

        nfraw = const.tile([P, 2048], BF16, name="nfraw")
        nfg = const.tile([P, 2048], BF16, name="nfg", align_bytes=64)
        nfc = const.tile([P, NB * 64], U32, name="nfc", align_bytes=64)
        nfs = const.tile([P, NB * 64], U8, name="nfs", align_bytes=64)
        relb = const.tile([P, NB * NR * 64], BF16, name="relb")
        identf = const.tile([P, P], F32, name="identf")
        ones = const.tile([P, NS], BF16, name="ones")
        wb_sb = const.tile([P, 4096], BF16, name="wb_sb")
        wbg = const.tile([P, 4096], BF16, name="wbg", align_bytes=64)
        wbc = const.tile([P, 1024], U32, name="wbc", align_bytes=64)
        wbs = const.tile([P, 1024], U8, name="wbs", align_bytes=64)

        nc.vector.memset(ones[:], 1.0)
        relrow = relation_features.rearrange("b r f -> (b r f)")
        wb_view = Wb.rearrange("(g p s) k -> p g (s k)", p=P, s=4)

        def load_wb(h):
            nc.sync.dma_start(
                out=wb_sb[:, h * 2048:(h + 1) * 2048],
                in_=wb_view[:, h, :],
            )

        def load_nf(b0, b1):
            nc.sync.dma_start(
                out=nfraw[:, b0 * 256:b1 * 256].rearrange("q (c x) -> q c x", c=2 * (b1 - b0)),
                in_=node_features[b0:b1].rearrange("b (u q e) d -> q (b u) (e d)", u=2, e=2),
            )

        def load_rel(b0, b1):
            nc.sync.dma_start(out=relb[:, b0 * 256:b1 * 256], in_=relrow[b0 * 256:b1 * 256].partition_broadcast(P))

        load_u(0, 0, 2)
        load_u(0, 2, 4)
        load_nf(0, 1)
        load_u(1, 0, 4)
        load_rel(0, 2)
        load_u(2, 0, 4)
        load_wb(0)
        load_u(3, 0, 4)
        load_wb(1)
        load_nf(1, 2)
        load_u(4, 0, 4)
        load_u(5, 0, 4)
        load_u(6, 0, 4)
        load_u(7, 0, 4)
        load_nf(2, 3)
        load_rel(2, 3)

        make_identity(nc, identf[:])

        def nf_regroup(b):
            dst = nfg[:, b * 256:(b + 1) * 256].rearrange("q (d t) -> q d t", t=4)
            src = nfraw[:, b * 256:(b + 1) * 256].rearrange("q (t d) -> q d t", t=4)
            if b == 0:
                nc.vector.tensor_copy(out=dst, in_=src)
            else:
                nc.gpsimd.tensor_scalar(out=dst, in0=src, scalar1=1.0, scalar2=0.0, op0=MULT, op1=ADD)

        def quant_nf(b):
            nc.vector.quantize_mx(
                out=nfc[:, b * 64:(b + 1) * 64].bitcast(FP8X4),
                scales=nfs[:, b * 64:(b + 1) * 64],
                in_=nfg[:, b * 256:(b + 1) * 256],
            )

        st = {"A": {}, "grp": {}, "cA": {}, "sA": {}, "N": {}, "sup": {}, "S": {}, "g2": {}, "c2": {}, "s2": {}, "D": {}, "rs": {}}

        def n_t(u):
            return 1 if u % 6 == 4 else 2

        def a_tr(u, h):
            bank_a = psum.tile([P, 512], F32, tag="A", bufs=3)
            for rr in range(2):
                for uu in range(2):
                    nc.tensor.transpose(
                        bank_a[:, (rr * 2 + uu) * 128:(rr * 2 + uu + 1) * 128],
                        rows(u, 2 * h + rr).bitcast(F32)[:, 128 * uu:128 * (uu + 1)],
                        identf[:],
                    )
            st["A"][(u, h)] = bank_a

        def a_exit(u, h):
            if u not in st["grp"]:
                grp = work.tile([P, 2048], BF16, tag="grp", bufs=3, align_bytes=64)
                st["grp"][u] = grp
            gw = st["grp"][u][:].bitcast(F32)
            nc.scalar.copy(
                out=gw[:, h * 512:(h + 1) * 512].rearrange("p (rr i u) -> p rr i u", rr=2, u=2),
                in_=st["A"][(u, h)][:].rearrange("p (rr u i) -> p rr i u", rr=2, u=2),
            )

        def q_a(u):
            c_a = work.tile([P, 512], U32, tag="cA", bufs=3, align_bytes=64)
            s_a = work.tile([P, 512], U8, tag="sA", bufs=3, align_bytes=64)
            st["cA"][u] = c_a
            st["sA"][u] = s_a
            nc.vector.quantize_mx(out=c_a[:].bitcast(FP8X4), scales=s_a[:], in_=st["grp"][u][:])

        def get_rs(u):
            if u not in st["rs"]:
                rs = work.tile([P, NR], F32, tag="rs", bufs=5)
                st["rs"][u] = rs
            return st["rs"][u]

        def rs_vec(u):
            rs = get_rs(u)
            for r in range(n_t(u), NR):
                junk = work.tile([P, 512], BF16, tag="junk", bufs=2)
                nc.vector.tensor_scalar(
                    out=junk[:],
                    in0=rows(u, r),
                    scalar1=1.0,
                    scalar2=0.0,
                    op0=MULT,
                    op1=ADD,
                    accum_out=rs[:, r:r + 1],
                )

        def rs_mm(u):
            bank_n = psum.tile([P, 256 + 2 * NS], F32, tag="N", bufs=2)
            st["N"][u] = bank_n
            gv = st["grp"][u][:].rearrange("p (r i t) -> p r i t", r=NR, t=4)
            for r in range(n_t(u)):
                for t in range(4):
                    nc.tensor.matmul(
                        out=bank_n[:, 256 + r * NS:256 + (r + 1) * NS],
                        lhsT=gv[:, r, :, t],
                        rhs=ones[:],
                        start=(t == 0),
                        stop=(t == 3),
                    )

        def b_mm(u):
            b, it = divmod(u, NT)
            bank_n = st["N"][u]
            for r in range(NR):
                nc.tensor.matmul_mx(
                    out=bank_n[:, r * 64:(r + 1) * 64],
                    lhsT=st["cA"][u][:, r * 128:(r + 1) * 128].bitcast(FP8X4),
                    lhsT_scale=st["sA"][u][:, r * 128:(r + 1) * 128],
                    rhs=nfc[:, b * 64:(b + 1) * 64].bitcast(FP8X4),
                    rhs_scale=nfs[:, b * 64:(b + 1) * 64],
                    start=True,
                    stop=True,
                )

        def get_sup(u):
            if u not in st["sup"]:
                sup = work.tile([P, 512], BF16, tag="sup", bufs=3, align_bytes=64)
                st["sup"][u] = sup
            return st["sup"][u][:].rearrange("p (r x) -> p r x", r=NR)

        def n_exit(u):
            nc.scalar.copy(
                out=get_sup(u)[:, :, 0:64],
                in_=st["N"][u][:, 0:256].rearrange("p (r d) -> p r d", r=NR),
            )

        def rs_exit(u):
            nc.scalar.copy(
                out=get_rs(u)[:, 0:n_t(u)],
                in_=st["N"][u][:, 256:256 + n_t(u) * NS].rearrange("p (r n) -> p r n", n=NS)[:, :, 0],
            )

        def rel(u):
            b = u // NT
            nc.gpsimd.tensor_tensor(
                out=get_sup(u)[:, :, 64:128],
                in0=relb[:, b * 256:(b + 1) * 256].rearrange("p (r f) -> p r f", r=NR),
                in1=st["rs"][u][:].rearrange("p (r n) -> p r n", n=1).to_broadcast([P, NR, 64]),
                op=MULT,
            )

        def s_tr(u):
            bank_s = psum.tile([P, 256], F32, tag="S", bufs=1)
            st["S"][u] = bank_s
            supw = st["sup"][u][:].bitcast(F32)
            for uu in range(2):
                nc.tensor.transpose(
                    bank_s[:, uu * 128:(uu + 1) * 128],
                    supw[:, uu * 128:(uu + 1) * 128],
                    identf[:],
                )

        def s_exit(u):
            g2 = work.tile([P, 512], BF16, tag="g2", bufs=3, align_bytes=64)
            st["g2"][u] = g2
            nc.scalar.copy(
                out=g2[:].bitcast(F32).rearrange("p (i u) -> p i u", u=2),
                in_=st["S"][u][:].rearrange("p (u i) -> p i u", u=2),
            )

        def q_s(u):
            c_2 = work.tile([P, P], U32, tag="c2", bufs=3, align_bytes=64)
            s_2 = work.tile([P, P], U8, tag="s2", bufs=3, align_bytes=64)
            st["c2"][u] = c_2
            st["s2"][u] = s_2
            nc.vector.quantize_mx(out=c_2[:].bitcast(FP8X4), scales=s_2[:], in_=st["g2"][u][:])

        def d_mm(u):
            banks = []
            for h in range(2):
                if u >= NU - 4 and u % 2 == 0:
                    bank_d = psum.tile([P, 512], F32, tag="A", bufs=3)
                else:
                    bank_d = psum.tile([P, 512], F32, tag="D", bufs=2)
                nc.tensor.matmul_mx(
                    out=bank_d[:],
                    lhsT=st["c2"][u][:].bitcast(FP8X4),
                    lhsT_scale=st["s2"][u][:],
                    rhs=wbc[:, h * 512:(h + 1) * 512].bitcast(FP8X4),
                    rhs_scale=wbs[:, h * 512:(h + 1) * 512],
                    start=True,
                    stop=True,
                )
                banks.append(bank_d)
            ost = work.tile([P, 1024], F32, tag="ost", bufs=10)
            st["D"][u] = (banks, ost)

        def d_exit(u, h):
            b, it = divmod(u, NT)
            banks, ost = st["D"][u]
            copy = nc.vector.tensor_copy if h else nc.scalar.copy
            copy(out=ost[:, h * 512:(h + 1) * 512], in_=banks[h][:])
            dst = out[b].rearrange("(p t) n -> p t n", t=NT)[:, it, :]
            if u == NU - 1:
                nc.sync.dma_start(out=dst[:, h * 512:(h + 1) * 512], in_=ost[:, h * 512:(h + 1) * 512])
            elif h == 1:
                nc.sync.dma_start(out=dst, in_=ost[:])

        wbank = {}

        def wb_tr(g):
            bank_w = psum.tile([P, 512], F32, tag="D", bufs=2)
            wbank[g] = bank_w
            wbw = wb_sb[:].bitcast(F32)
            for nn in range(2):
                for uu in range(2):
                    col = (2 * g + nn) * 256 + uu * 128
                    nc.tensor.transpose(
                        bank_w[:, (nn * 2 + uu) * 128:(nn * 2 + uu + 1) * 128],
                        wbw[:, col:col + 128],
                        identf[:],
                    )

        def wb_exit(g, copy):
            h, j = divmod(g, 2)
            wide = wbg[:, h * 2048:(h + 1) * 2048].bitcast(F32).rearrange("p (n s u) -> p n s u", s=4, u=2)
            copy(
                out=wide[:, :, 2 * j:2 * j + 2, :],
                in_=wbank[g][:].rearrange("p (s u n) -> p n s u", s=2, u=2),
            )

        def wb_quant(h):
            nc.vector.quantize_mx(
                out=wbc[:, h * 512:(h + 1) * 512].bitcast(FP8X4),
                scales=wbs[:, h * 512:(h + 1) * 512],
                in_=wbg[:, h * 2048:(h + 1) * 2048],
            )

        def ok(u):
            return 0 <= u < NU


        for k in range(NU + LAG):
            if k < 4 * (NB - NE):
                load_r(NE + k // 4, k % 4)
            if k == 4:
                load_nf(3, NB)
                load_rel(3, NB)
            if ok(k):
                a_tr(k, 0)
            if ok(k):
                a_tr(k, 1)
            if ok(k - 3):
                s_tr(k - 3)
            if k in (2, 3):
                wb_tr(2 * (k - 2))
                wb_tr(2 * (k - 2) + 1)
            if k == 0:
                nf_regroup(0)
                quant_nf(0)
            if k % 4 == 0 and 1 <= k // 4 < NB:
                quant_nf(k // 4)
            if ok(k - 5):
                d_exit(k - 5, 0)
            if ok(k - 2):
                rs_exit(k - 2)
            if ok(k - 2):
                n_exit(k - 2)
            if ok(k):
                a_exit(k, 0)
            if ok(k):
                a_exit(k, 1)
            if ok(k - 3):
                s_exit(k - 3)
            if ok(k - 2):
                rel(k - 2)
            if ok(k - 1):
                q_a(k - 1)
            if ok(k - 4):
                q_s(k - 4)
            if k in (3, 4):
                wb_quant(k - 3)
            if ok(k - 5):
                d_exit(k - 5, 1)
            if ok(k):
                rs_vec(k)
            if ok(k - 1):
                rs_mm(k - 1)
            if ok(k - 4):
                d_mm(k - 4)
            if ok(k - 1):
                b_mm(k - 1)
            if k % 4 == 2 and k // 4 + 1 < NB:
                nf_regroup(k // 4 + 1)
            if k in (2, 3):
                wb_exit(2 * (k - 2), nc.scalar.copy)
                wb_exit(2 * (k - 2) + 1, nc.scalar.copy)
